import numpy as np
import ml_dtypes


def mxq(x, axis, fmt="e4m3"):
    dtype, down = {"e4m3": (ml_dtypes.float8_e4m3fn, 7), "e5m2": (ml_dtypes.float8_e5m2, 14)}[fmt]
    v = np.moveaxis(np.asarray(x, np.float32).astype(ml_dtypes.bfloat16).astype(np.float64), axis, -1)
    blocks = v.reshape(v.shape[:-1] + (-1, 32))
    amax = np.abs(blocks).max(-1, keepdims=True)
    byte = np.maximum(np.where(amax > 0, np.frexp(amax)[1] - 1 + 127, 0) - down, 1)
    scale = np.exp2(byte - 127.0)
    codes = (blocks / scale).astype(np.float32).astype(dtype).astype(np.float64)
    return np.moveaxis((codes * scale).reshape(v.shape), -1, axis)


WIDE = False


def mx_kscale(k):
    if not WIDE:
        return np.ones(k)
    levels = np.array([10, -10, 5, -5, 0])
    if k % 512:
        return np.exp2(np.random.permutation(np.resize(levels, k // 32))).repeat(32)
    a = np.empty((k // 512, 16))
    for p in range(k // 512):
        a[p, :8] = np.random.permutation(np.resize(levels, 8))
        for g in range(8):
            far = levels[np.abs(levels - a[p, g]) >= 10]
            a[p, g + 8] = far[np.random.randint(len(far))]
    return np.exp2(a.ravel()).repeat(32)


BF16 = ml_dtypes.bfloat16


def bf(x):
    return np.asarray(x, np.float32).astype(BF16)


def f64(x):
    return np.asarray(x).astype(np.float64)


N, MI0, MI1, MS, MG, MO0, MO1, DV = 4096, 128, 128, 512, 512, 256, 256, 3
EPS = 1e-5


def irlin_mx(x, mul0, mul1, w0, w1):
    n = x.shape[0]
    x0 = x[:, :mul0]
    x1 = x[:, mul0:].reshape(n, mul1, DV).transpose(0, 2, 1)
    y0 = (mxq(x0, 1, "e4m3") @ mxq(w0, 0, "e4m3")) * (1.0 / np.sqrt(mul0))
    y1 = (mxq(x1, 2, "e4m3") @ mxq(w1, 0, "e4m3")).transpose(0, 2, 1) * (1.0 / np.sqrt(mul1))
    return np.concatenate([y0, y1.reshape(n, -1)], axis=-1)


def irlin_plain(x, mul0, mul1, w0, w1):
    n = x.shape[0]
    x0 = x[:, :mul0]
    x1 = x[:, mul0:].reshape(n, mul1, DV).transpose(0, 2, 1)
    y0 = (x0 @ w0) * (1.0 / np.sqrt(mul0))
    y1 = (x1 @ w1).transpose(0, 2, 1) * (1.0 / np.sqrt(mul1))
    return np.concatenate([y0, y1.reshape(n, -1)], axis=-1)


def batchnorm(x, w, b):
    n = x.shape[0]
    s = x[:, :MO0]
    v = x[:, MO0:].reshape(n, MO1, DV)
    s = s - s.mean(0)
    s_inv = 1.0 / np.sqrt((s * s).mean(0) + EPS)
    s = s * (s_inv * w[:MO0]) + b
    v_inv = 1.0 / np.sqrt((v * v).mean(-1).mean(0) + EPS)
    v = v * (v_inv * w[MO0:])[None, :, None]
    return np.concatenate([s, v.reshape(n, -1)], axis=-1)


def setup_inputs():
    s0, s1 = mx_kscale(MS), mx_kscale(MG)
    h0 = (0.1 + 0.3 * np.random.standard_normal((N, MS))) * s0
    h1 = 0.28 * np.random.standard_normal((N, MG, DV)) * s1[None, :, None]
    return {"h2": bf(np.concatenate([h0, h1.reshape(N, -1)], axis=-1)),
            "features": bf(np.random.standard_normal((N, MI0 + DV * MI1))),
            "lin3_W0": bf(np.random.standard_normal((MS, MO0)) / s0[:, None]),
            "lin3_W1": bf(np.random.standard_normal((MG, MO1)) / s1[:, None]),
            "byp_W0": bf(np.random.standard_normal((MI0, MO0))),
            "byp_W1": bf(np.random.standard_normal((MI1, MO1))),
            "bn_weight": bf(1.0 + 0.1 * np.random.standard_normal(MO0 + MO1)),
            "bn_bias": bf(0.1 * np.random.standard_normal(MO0))}


def reference(h2, features, lin3_W0, lin3_W1, byp_W0, byp_W1, bn_weight, bn_bias):
    out = irlin_mx(f64(h2), MS, MG, f64(lin3_W0), f64(lin3_W1))
    out = out + irlin_plain(f64(features), MI0, MI1, f64(byp_W0), f64(byp_W1))
    return batchnorm(out, f64(bn_weight), f64(bn_bias))

@@ -1,0 +1,305 @@
+from contextlib import ExitStack
+import math
+
+import concourse.mybir as mybir
+from concourse.masks import make_identity
+
+F32 = mybir.dt.float32
+BF16 = mybir.dt.bfloat16
+U32 = mybir.dt.uint32
+U8 = mybir.dt.uint8
+FP8X4 = mybir.dt.float8_e4m3fn_x4
+ALU = mybir.AluOpType
+ACT = mybir.ActivationFunctionType
+
+P = 128
+NODES = 4096
+DV = 3
+SECTIONS = 1 + DV
+HID = 512
+INP = 128
+OUTC = 256
+HALVES = OUTC // P
+GROUP = 512
+J = GROUP // P
+GROUPS = NODES // GROUP
+STATS = 6
+EPS = 1e-5
+
+FLOPS = 2 * NODES * SECTIONS * OUTC * (HID + INP)
+
+
+def quantise_weight(nc, pool, w, label):
+    raw = pool.tile([P, 4, OUTC], BF16, name="w_raw")
+    nc.scalar.dma_start(out=raw[:], in_=w.rearrange("(p t) c -> p t c", t=4))
+    grouped = pool.tile([P, OUTC, 4], BF16, name="w_grouped", align_bytes=64)
+    nc.vector.tensor_copy(out=grouped[:], in_=raw[:].rearrange("p t c -> p c t"))
+    codes = pool.tile([P, OUTC], U32, name=label + "_codes", align_bytes=64)
+    scales = pool.tile([P, OUTC], U8, name=label + "_scales", align_bytes=64)
+    nc.vector.quantize_mx(
+        out=codes[:].bitcast(FP8X4),
+        scales=scales[:],
+        in_=grouped[:].rearrange("p c t -> p (c t)"),
+    )
+    return codes, scales
+
+
+def tile_feedforward_pb_t_kernel(
+    tc, h2, features, lin3_W0, lin3_W1, byp_W0, byp_W1, bn_weight, bn_bias, out
+):
+    nc = tc.nc
+    with ExitStack() as whole:
+        consts = whole.enter_context(tc.tile_pool(name="consts", bufs=1))
+        y_pool = whole.enter_context(tc.tile_pool(name="y", bufs=1))
+
+        ident_f32 = consts.tile([P, P], F32)
+        make_identity(nc, ident_f32[:])
+        ident_bf16 = consts.tile([P, P], BF16)
+        make_identity(nc, ident_bf16[:])
+
+        warm = consts.tile([P, 1], F32)
+        nc.vector.memset(warm[:], 1.0)
+        nc.scalar.sqrt(out=warm[:], in_=warm[:])
+
+        lin_w = [
+            quantise_weight(nc, consts, lin3_W0, "w0"),
+            quantise_weight(nc, consts, lin3_W1, "w1"),
+        ]
+        byp_w = []
+        for label, w in (("byp0", byp_W0), ("byp1", byp_W1)):
+            w_sb = consts.tile([P, OUTC], BF16, name=label)
+            nc.scalar.dma_start(out=w_sb[:], in_=w)
+            byp_w.append(w_sb)
+
+        bn_rows = consts.tile([P, P], BF16)
+        nc.vector.memset(bn_rows[:], 0.0)
+        nc.scalar.dma_start(out=bn_rows[0:4, :], in_=bn_weight.rearrange("(r c) -> r c", c=P))
+        nc.scalar.dma_start(out=bn_rows[4:6, :], in_=bn_bias.rearrange("(r c) -> r c", c=P))
+        bn_cols = consts.tile([P, 6], F32)
+
+        y = [y_pool.tile([P, HALVES, SECTIONS, GROUP], F32, name="y%d" % g) for g in range(GROUPS)]
+        stats_scal = consts.tile([P, HALVES, GROUPS, STATS], F32)
+        stats_vec = consts.tile([P, HALVES, GROUPS * DV, STATS], F32)
+
+        with ExitStack() as phase1:
+            stage = phase1.enter_context(tc.tile_pool(name="stage", bufs=2))
+            work = phase1.enter_context(tc.tile_pool(name="work", bufs=3))
+            psum_x = phase1.enter_context(tc.psum_pool(name="psum_x", bufs=2))
+            psum_f = phase1.enter_context(tc.psum_pool(name="psum_f", bufs=2))
+            psum_mx = phase1.enter_context(tc.psum_pool(name="psum_mx", bufs=2))
+            psum_byp = phase1.enter_context(tc.psum_pool(name="psum_byp", bufs=2))
+
+            bn_ps = psum_f.tile([P, P], BF16, tag="feat_ps")
+            nc.tensor.transpose(bn_ps[:], bn_rows[:], ident_bf16[:])
+            nc.vector.tensor_copy(out=bn_cols[:], in_=bn_ps[:, 0:6])
+
+            loaded = {}
+
+            def load(g):
+                rows = slice(g * GROUP, (g + 1) * GROUP)
+                h2_scal = stage.tile([P, J, HID], BF16, name="h2_scal")
+                nc.sync.dma_start(
+                    out=h2_scal[:], in_=h2[rows, 0:HID].rearrange("(p j) k -> p j k", j=J)
+                )
+                feat = stage.tile([P, J, SECTIONS * INP], BF16, name="feat")
+                nc.sync.dma_start(
+                    out=feat[:], in_=features[rows, :].rearrange("(p j) k -> p j k", j=J)
+                )
+                h2_vec = stage.tile([P, J, DV * HID], BF16, name="h2_vec")
+                nc.sync.dma_start(
+                    out=h2_vec[:], in_=h2[rows, HID:].rearrange("(p j) k -> p j k", j=J)
+                )
+                loaded[g] = (h2_scal, feat, h2_vec)
+
+            def prepare(g, s):
+                h2_scal, feat, h2_vec = loaded[g]
+                if s == 0:
+                    hidden = h2_scal
+                else:
+                    hidden = stage.tile([P, J, HID], BF16, name="h2_comp", bufs=5)
+                grouped = work.tile([P, GROUP, 2], F32, name="grouped", align_bytes=64)
+                for half in range(2):
+                    if s > 0:
+                        for j in range(2 * half, 2 * half + 2):
+                            nc.gpsimd.tensor_scalar(
+                                out=hidden[:, j, :].rearrange("p (u q e) -> p u q e", u=2, e=2),
+                                in0=h2_vec[:, j, :].rearrange(
+                                    "p (q u e d) -> p d u q e", u=2, e=2, d=DV
+                                )[:, s - 1],
+                                scalar1=1.0,
+                                scalar2=0.0,
+                                op0=ALU.mult,
+                                op1=ALU.add,
+                            )
+                    hid_ps = psum_x.tile([P, 2, 2 * P], F32, name="hid_ps")
+                    for jj in range(2):
+                        words = hidden[:, 2 * half + jj, :].bitcast(F32)
+                        for u in range(2):
+                            plane = words[:, u::2] if s == 0 else words[:, u * P : (u + 1) * P]
+                            nc.tensor.transpose(
+                                hid_ps[:, u, jj * P : (jj + 1) * P], plane, ident_f32[:]
+                            )
+                    nc.scalar.copy(
+                        out=grouped[:, half * 2 * P : (half + 1) * 2 * P, :],
+                        in_=hid_ps[:].rearrange("p u n -> p n u"),
+                    )
+                codes = work.tile([P, GROUP], U32, name="codes", align_bytes=64)
+                scales = work.tile([P, GROUP], U8, name="scales", align_bytes=64)
+                nc.vector.quantize_mx(
+                    out=codes[:].bitcast(FP8X4),
+                    scales=scales[:],
+                    in_=grouped[:].rearrange("p n w -> p (n w)").bitcast(BF16),
+                )
+                feat_ps = psum_f.tile([P, GROUP], BF16, name="feat_ps")
+                for j in range(J):
+                    if s == 0:
+                        cols = feat[:, j, 0:INP]
+                    else:
+                        cols = feat[:, j, INP:].rearrange("p (i d) -> p d i", d=DV)[:, s - 1]
+                    nc.tensor.transpose(feat_ps[:, j * P : (j + 1) * P], cols, ident_bf16[:])
+                featT = work.tile([P, GROUP], BF16, name="featT")
+                nc.scalar.copy(out=featT[:], in_=feat_ps[:])
+                return codes, scales, featT
+
+            def multiply(g, s, operands):
+                codes, scales, featT = operands
+                kind = min(s, 1)
+                w_codes, w_scales = lin_w[kind]
+                bypass = []
+                for h in range(HALVES):
+                    chans = slice(h * P, (h + 1) * P)
+                    byp_ps = psum_byp.tile([P, GROUP], F32, name="byp_ps")
+                    nc.tensor.matmul(
+                        out=byp_ps[:], lhsT=byp_w[kind][:, chans], rhs=featT[:], start=True, stop=True
+                    )
+                    byp_sb = work.tile([P, GROUP], F32, name="byp_sb")
+                    nc.scalar.mul(out=byp_sb[:], in_=byp_ps[:], mul=1.0 / math.sqrt(INP))
+                    bypass.append(byp_sb)
+                for h in range(HALVES):
+                    chans = slice(h * P, (h + 1) * P)
+                    mx_ps = psum_mx.tile([P, GROUP], F32, name="mx_ps")
+                    nc.tensor.matmul_mx(
+                        out=mx_ps[:],
+                        lhsT=w_codes[:, chans].bitcast(FP8X4),
+                        lhsT_scale=w_scales[:, chans],
+                        rhs=codes[:].bitcast(FP8X4),
+                        rhs_scale=scales[:],
+                        start=True,
+                        stop=True,
+                    )
+                    nc.vector.scalar_tensor_tensor(
+                        out=y[g][:, h, s, :],
+                        in0=mx_ps[:],
+                        scalar=1.0 / math.sqrt(HID),
+                        in1=bypass[h][:],
+                        op0=ALU.mult,
+                        op1=ALU.add,
+                    )
+                for h in range(HALVES):
+                    if s == 0:
+                        chunk = stats_scal[:, h, g, :]
+                    else:
+                        chunk = stats_vec[:, h, g * DV + s - 1, :]
+                    nc.vector.bn_stats(out=chunk, in_=y[g][:, h, s, :])
+
+            todo = [(g, s) for g in range(GROUPS) for s in range(SECTIONS)]
+            load(0)
+            load(1)
+            ready = prepare(*todo[0])
+            for i in range(1, len(todo)):
+                g, s = todo[i]
+                if s == 0 and g + 1 < GROUPS:
+                    load(g + 1)
+                following = prepare(g, s)
+                multiply(todo[i - 1][0], todo[i - 1][1], ready)
+                ready = following
+            multiply(todo[-1][0], todo[-1][1], ready)
+
+        moments = consts.tile([P, 2 * HALVES, 2], F32)
+        for h in range(HALVES):
+            nc.vector.bn_aggr(
+                out=moments[:, h, :], in_=stats_scal[:, h].rearrange("p c s -> p (c s)")
+            )
+            nc.vector.bn_aggr(
+                out=moments[:, HALVES + h, :], in_=stats_vec[:, h].rearrange("p c s -> p (c s)")
+            )
+        mean_sq = consts.tile([P, HALVES], F32)
+        nc.vector.tensor_mul(out=mean_sq[:], in0=moments[:, HALVES:, 0], in1=moments[:, HALVES:, 0])
+        spread = consts.tile([P, 2 * HALVES], F32)
+        nc.vector.tensor_scalar_add(out=spread[:, 0:HALVES], in0=moments[:, 0:HALVES, 1], scalar1=EPS)
+        nc.vector.scalar_tensor_tensor(
+            out=spread[:, HALVES:],
+            in0=moments[:, HALVES:, 1],
+            scalar=EPS,
+            in1=mean_sq[:],
+            op0=ALU.add,
+            op1=ALU.add,
+        )
+        root = consts.tile([P, 2 * HALVES], F32)
+        nc.scalar.sqrt(out=root[:], in_=spread[:])
+        scale = consts.tile([P, 2 * HALVES], F32)
+        nc.vector.reciprocal(out=scale[:], in_=root[:])
+        nc.vector.tensor_mul(out=scale[:], in0=scale[:], in1=bn_cols[:, 0 : 2 * HALVES])
+        shift = consts.tile([P, 2 * HALVES], F32)
+        nc.vector.memset(shift[:], 0.0)
+        scaled_mean = consts.tile([P, HALVES], F32)
+        nc.vector.tensor_mul(out=scaled_mean[:], in0=moments[:, 0:HALVES, 0], in1=scale[:, 0:HALVES])
+        nc.vector.tensor_sub(
+            out=shift[:, 0:HALVES], in0=bn_cols[:, 2 * HALVES : 3 * HALVES], in1=scaled_mean[:]
+        )
+
+        with ExitStack() as phase2:
+            rows_pool = phase2.enter_context(tc.tile_pool(name="rows", bufs=3))
+            psum_s = phase2.enter_context(tc.psum_pool(name="psum_s", bufs=2))
+            psum_v = phase2.enter_context(tc.psum_pool(name="psum_v", bufs=6))
+
+            def normalise(g):
+                for h in range(HALVES):
+                    nc.scalar.activation(
+                        out=y[g][:, h, 0, :],
+                        in_=y[g][:, h, 0, :],
+                        func=ACT.Identity,
+                        scale=scale[:, h : h + 1],
+                        bias=shift[:, h : h + 1],
+                    )
+                    b = HALVES + h
+                    nc.gpsimd.tensor_scalar(
+                        out=y[g][:, h, 1:, :],
+                        in0=y[g][:, h, 1:, :],
+                        scalar1=scale[:, b : b + 1],
+                        scalar2=shift[:, b : b + 1],
+                        op0=ALU.mult,
+                        op1=ALU.add,
+                    )
+
+            def store(g, half):
+                rows_sb = rows_pool.tile([P, 2, SECTIONS * OUTC], F32, name="rows_sb")
+                scal_ps = psum_s.tile([P, 2, HALVES, P], F32, name="scal_ps")
+                for jj in range(2):
+                    nodes = slice((2 * half + jj) * P, (2 * half + jj + 1) * P)
+                    for h in range(HALVES):
+                        nc.tensor.transpose(scal_ps[:, jj, h, :], y[g][:, h, 0, nodes], ident_f32[:])
+                nc.vector.tensor_copy(
+                    out=rows_sb[:, :, 0:OUTC], in_=scal_ps[:].rearrange("p j h c -> p j (h c)")
+                )
+                for jj in range(2):
+                    nodes = slice((2 * half + jj) * P, (2 * half + jj + 1) * P)
+                    for h in range(HALVES):
+                        vec_ps = psum_v.tile([P, DV, P], F32, name="vec_ps")
+                        for d in range(DV):
+                            nc.tensor.transpose(vec_ps[:, d, :], y[g][:, h, 1 + d, nodes], ident_f32[:])
+                        first = OUTC + h * DV * P
+                        dest = rows_sb[:, jj, first : first + DV * P].rearrange("p (o d) -> p o d", d=DV)
+                        if h == 0:
+                            nc.vector.tensor_copy(out=dest, in_=vec_ps[:].rearrange("p d o -> p o d"))
+                        else:
+                            nc.scalar.copy(out=dest, in_=vec_ps[:].rearrange("p d o -> p o d"))
+                group_rows = out[g * GROUP : (g + 1) * GROUP, :].rearrange("(p j) c -> p j c", j=J)
+                nc.sync.dma_start(out=group_rows[:, 2 * half : 2 * half + 2, :], in_=rows_sb[:])
+
+            normalise(0)
+            for g in range(GROUPS):
+                if g + 1 < GROUPS:
+                    normalise(g + 1)
+                for half in range(2):
+                    store(g, half)

@@ -25,6 +25,7 @@ J = GROUP // P
 GROUPS = NODES // GROUP
 STATS = 6
 EPS = 1e-5
+EARLY = 4
 
 FLOPS = 2 * NODES * SECTIONS * OUTC * (HID + INP)
 
@@ -51,6 +52,8 @@ def tile_feedforward_pb_t_kernel(
     with ExitStack() as whole:
         consts = whole.enter_context(tc.tile_pool(name="consts", bufs=1))
         y_pool = whole.enter_context(tc.tile_pool(name="y", bufs=1))
+        scal_in = whole.enter_context(tc.tile_pool(name="scal_in", bufs=2))
+        work = whole.enter_context(tc.tile_pool(name="work", bufs=2))
 
         ident_f32 = consts.tile([P, P], F32)
         make_identity(nc, ident_f32[:])
@@ -77,229 +80,306 @@ def tile_feedforward_pb_t_kernel(
         nc.scalar.dma_start(out=bn_rows[4:6, :], in_=bn_bias.rearrange("(r c) -> r c", c=P))
         bn_cols = consts.tile([P, 6], F32)
 
-        y = [y_pool.tile([P, HALVES, SECTIONS, GROUP], F32, name="y%d" % g) for g in range(GROUPS)]
+        y_scal = [y_pool.tile([P, HALVES, GROUP], F32, name="ys%d" % g) for g in range(GROUPS)]
+        y_vec = [y_pool.tile([P, HALVES, DV, GROUP], F32, name="yv%d" % g) for g in range(GROUPS)]
         stats_scal = consts.tile([P, HALVES, GROUPS, STATS], F32)
         stats_vec = consts.tile([P, HALVES, GROUPS * DV, STATS], F32)
 
-        with ExitStack() as phase1:
-            stage = phase1.enter_context(tc.tile_pool(name="stage", bufs=2))
-            work = phase1.enter_context(tc.tile_pool(name="work", bufs=3))
-            psum_x = phase1.enter_context(tc.psum_pool(name="psum_x", bufs=2))
-            psum_f = phase1.enter_context(tc.psum_pool(name="psum_f", bufs=2))
-            psum_mx = phase1.enter_context(tc.psum_pool(name="psum_mx", bufs=2))
-            psum_byp = phase1.enter_context(tc.psum_pool(name="psum_byp", bufs=2))
+        loaded = {}
 
-            bn_ps = psum_f.tile([P, P], BF16, tag="feat_ps")
+        def load_scal(g):
+            rows = slice(g * GROUP, (g + 1) * GROUP)
+            hidden = scal_in.tile([P, J, HID], BF16, name="h2_scal")
+            nc.sync.dma_start(
+                out=hidden[:], in_=h2[rows, 0:HID].rearrange("(p j) k -> p j k", j=J)
+            )
+            feat = scal_in.tile([P, J, INP], BF16, name="feat_scal")
+            nc.sync.dma_start(
+                out=feat[:], in_=features[rows, 0:INP].rearrange("(p j) k -> p j k", j=J)
+            )
+            loaded[(g, 0)] = (hidden, feat)
+
+        def load_vec(g, vec_in):
+            rows = slice(g * GROUP, (g + 1) * GROUP)
+            hidden = vec_in.tile([P, J, DV * HID], BF16, name="h2_vec")
+            nc.sync.dma_start(
+                out=hidden[:], in_=h2[rows, HID:].rearrange("(p j) k -> p j k", j=J)
+            )
+            feat = vec_in.tile([P, J, DV * INP], BF16, name="feat_vec")
+            nc.sync.dma_start(
+                out=feat[:], in_=features[rows, INP:].rearrange("(p j) k -> p j k", j=J)
+            )
+            for s in range(1, SECTIONS):
+                loaded[(g, s)] = (hidden, feat)
+
+        def prepare(g, s, banks, vec_in):
+            source, feat = loaded[(g, s)]
+            hidden = source if s == 0 else vec_in.tile([P, J, HID], BF16, name="h2_comp")
+            grouped = work.tile([P, GROUP, 2], F32, name="grouped", align_bytes=64)
+            for half in range(2):
+                hid_ps = banks["x"].tile([P, 2, 2 * P], F32, name="hid_ps")
+                if s > 0:
+                    pair = slice(2 * half, 2 * half + 2)
+                    nc.gpsimd.tensor_scalar(
+                        out=hidden[:, pair, :],
+                        in0=source[:, pair, :].rearrange("p j (i d) -> p d j i", d=DV)[:, s - 1],
+                        scalar1=1.0,
+                        scalar2=0.0,
+                        op0=ALU.mult,
+                        op1=ALU.add,
+                    )
+                for jj in range(2):
+                    words = hidden[:, 2 * half + jj, :].bitcast(F32)
+                    for u in range(2):
+                        nc.tensor.transpose(
+                            hid_ps[:, u, jj * P : (jj + 1) * P], words[:, u::2], ident_f32[:]
+                        )
+                nc.scalar.copy(
+                    out=grouped[:, half * 2 * P : (half + 1) * 2 * P, :],
+                    in_=hid_ps[:].rearrange("p u n -> p n u"),
+                )
+            codes = work.tile([P, GROUP], U32, name="codes", align_bytes=64)
+            scales = work.tile([P, GROUP], U8, name="scales", align_bytes=64)
+            nc.vector.quantize_mx(
+                out=codes[:].bitcast(FP8X4),
+                scales=scales[:],
+                in_=grouped[:].rearrange("p n w -> p (n w)").bitcast(BF16),
+            )
+            feat_ps = banks["f"].tile([P, GROUP], BF16, name="feat_ps")
+            for j in range(J):
+                cols = feat[:, j, :]
+                if s > 0:
+                    cols = cols.rearrange("p (i d) -> p d i", d=DV)[:, s - 1]
+                nc.tensor.transpose(feat_ps[:, j * P : (j + 1) * P], cols, ident_bf16[:])
+            featT = work.tile([P, GROUP], BF16, name="featT", bufs=3)
+            nc.scalar.copy(out=featT[:], in_=feat_ps[:])
+            return codes, scales, featT
+
+        def multiply(g, s, operands, banks):
+            codes, scales, featT = operands
+            kind = min(s, 1)
+            w_codes, w_scales = lin_w[kind]
+            bypass = []
+            for h in range(HALVES):
+                chans = slice(h * P, (h + 1) * P)
+                byp_ps = banks["byp"].tile([P, GROUP], F32, name="byp_ps")
+                nc.tensor.matmul(
+                    out=byp_ps[:], lhsT=byp_w[kind][:, chans], rhs=featT[:], start=True, stop=True
+                )
+                byp_sb = work.tile([P, GROUP], F32, name="byp_sb", bufs=4)
+                nc.scalar.mul(out=byp_sb[:], in_=byp_ps[:], mul=1.0 / math.sqrt(INP))
+                bypass.append(byp_sb)
+            for h in range(HALVES):
+                chans = slice(h * P, (h + 1) * P)
+                mx_ps = banks["mx"].tile([P, GROUP], F32, name="mx_ps")
+                nc.tensor.matmul_mx(
+                    out=mx_ps[:],
+                    lhsT=w_codes[:, chans].bitcast(FP8X4),
+                    lhsT_scale=w_scales[:, chans],
+                    rhs=codes[:].bitcast(FP8X4),
+                    rhs_scale=scales[:],
+                    start=True,
+                    stop=True,
+                )
+                y = y_scal[g][:, h, :] if s == 0 else y_vec[g][:, h, s - 1, :]
+                nc.vector.scalar_tensor_tensor(
+                    out=y,
+                    in0=mx_ps[:],
+                    scalar=1.0 / math.sqrt(HID),
+                    in1=bypass[h][:],
+                    op0=ALU.mult,
+                    op1=ALU.add,
+                )
+            for h in range(HALVES):
+                if s == 0:
+                    nc.vector.bn_stats(out=stats_scal[:, h, g, :], in_=y_scal[g][:, h, :])
+                else:
+                    nc.vector.bn_stats(
+                        out=stats_vec[:, h, g * DV + s - 1, :], in_=y_vec[g][:, h, s - 1, :]
+                    )
+
+        def norm_scale(stats, kind):
+            moments = consts.tile([P, HALVES, 2], F32, name="moments%d" % kind)
+            for h in range(HALVES):
+                nc.vector.bn_aggr(out=moments[:, h, :], in_=stats[:, h].rearrange("p c s -> p (c s)"))
+            spread = consts.tile([P, HALVES], F32, name="spread%d" % kind)
+            if kind == 0:
+                nc.vector.tensor_scalar_add(out=spread[:], in0=moments[:, :, 1], scalar1=EPS)
+            else:
+                mean_sq = consts.tile([P, HALVES], F32)
+                nc.vector.tensor_mul(out=mean_sq[:], in0=moments[:, :, 0], in1=moments[:, :, 0])
+                nc.vector.scalar_tensor_tensor(
+                    out=spread[:],
+                    in0=moments[:, :, 1],
+                    scalar=EPS,
+                    in1=mean_sq[:],
+                    op0=ALU.add,
+                    op1=ALU.add,
+                )
+            root = consts.tile([P, HALVES], F32, name="root%d" % kind)
+            nc.scalar.sqrt(out=root[:], in_=spread[:])
+            inverse = consts.tile([P, HALVES], F32, name="inverse%d" % kind)
+            nc.vector.reciprocal(out=inverse[:], in_=root[:])
+            scale = consts.tile([P, HALVES], F32, name="scale%d" % kind)
+            nc.vector.tensor_mul(
+                out=scale[:], in0=inverse[:], in1=bn_cols[:, kind * HALVES : (kind + 1) * HALVES]
+            )
+            return moments, scale
+
+        todo = []
+        for g in range(GROUPS):
+            if g % 2 == 0 and g // 2 < EARLY:
+                todo.append((g // 2, 0))
+            todo += [(g, s) for s in range(1, SECTIONS)]
+        first_late = len(todo)
+        todo += [(g, 0) for g in range(EARLY, GROUPS)]
+
+        with ExitStack() as part_a:
+            vec_in = part_a.enter_context(tc.tile_pool(name="vec_in", bufs=3))
+            banks_a = {
+                "x": part_a.enter_context(tc.psum_pool(name="psum_xa", bufs=2)),
+                "f": part_a.enter_context(tc.psum_pool(name="psum_fa", bufs=2)),
+                "mx": part_a.enter_context(tc.psum_pool(name="psum_mxa", bufs=2)),
+                "byp": part_a.enter_context(tc.psum_pool(name="psum_bypa", bufs=2)),
+            }
+            bn_ps = banks_a["f"].tile([P, P], BF16, tag="feat_ps")
             nc.tensor.transpose(bn_ps[:], bn_rows[:], ident_bf16[:])
             nc.vector.tensor_copy(out=bn_cols[:], in_=bn_ps[:, 0:6])
 
-            loaded = {}
-
-            def load(g):
-                rows = slice(g * GROUP, (g + 1) * GROUP)
-                h2_scal = stage.tile([P, J, HID], BF16, name="h2_scal")
-                nc.sync.dma_start(
-                    out=h2_scal[:], in_=h2[rows, 0:HID].rearrange("(p j) k -> p j k", j=J)
-                )
-                feat = stage.tile([P, J, SECTIONS * INP], BF16, name="feat")
-                nc.sync.dma_start(
-                    out=feat[:], in_=features[rows, :].rearrange("(p j) k -> p j k", j=J)
-                )
-                h2_vec = stage.tile([P, J, DV * HID], BF16, name="h2_vec")
-                nc.sync.dma_start(
-                    out=h2_vec[:], in_=h2[rows, HID:].rearrange("(p j) k -> p j k", j=J)
-                )
-                loaded[g] = (h2_scal, feat, h2_vec)
-
-            def prepare(g, s):
-                h2_scal, feat, h2_vec = loaded[g]
-                if s == 0:
-                    hidden = h2_scal
-                else:
-                    hidden = stage.tile([P, J, HID], BF16, name="h2_comp", bufs=5)
-                grouped = work.tile([P, GROUP, 2], F32, name="grouped", align_bytes=64)
-                for half in range(2):
-                    if s > 0:
-                        for j in range(2 * half, 2 * half + 2):
-                            nc.gpsimd.tensor_scalar(
-                                out=hidden[:, j, :].rearrange("p (u q e) -> p u q e", u=2, e=2),
-                                in0=h2_vec[:, j, :].rearrange(
-                                    "p (q u e d) -> p d u q e", u=2, e=2, d=DV
-                                )[:, s - 1],
-                                scalar1=1.0,
-                                scalar2=0.0,
-                                op0=ALU.mult,
-                                op1=ALU.add,
-                            )
-                    hid_ps = psum_x.tile([P, 2, 2 * P], F32, name="hid_ps")
-                    for jj in range(2):
-                        words = hidden[:, 2 * half + jj, :].bitcast(F32)
-                        for u in range(2):
-                            plane = words[:, u::2] if s == 0 else words[:, u * P : (u + 1) * P]
-                            nc.tensor.transpose(
-                                hid_ps[:, u, jj * P : (jj + 1) * P], plane, ident_f32[:]
-                            )
-                    nc.scalar.copy(
-                        out=grouped[:, half * 2 * P : (half + 1) * 2 * P, :],
-                        in_=hid_ps[:].rearrange("p u n -> p n u"),
-                    )
-                codes = work.tile([P, GROUP], U32, name="codes", align_bytes=64)
-                scales = work.tile([P, GROUP], U8, name="scales", align_bytes=64)
-                nc.vector.quantize_mx(
-                    out=codes[:].bitcast(FP8X4),
-                    scales=scales[:],
-                    in_=grouped[:].rearrange("p n w -> p (n w)").bitcast(BF16),
-                )
-                feat_ps = psum_f.tile([P, GROUP], BF16, name="feat_ps")
-                for j in range(J):
-                    if s == 0:
-                        cols = feat[:, j, 0:INP]
-                    else:
-                        cols = feat[:, j, INP:].rearrange("p (i d) -> p d i", d=DV)[:, s - 1]
-                    nc.tensor.transpose(feat_ps[:, j * P : (j + 1) * P], cols, ident_bf16[:])
-                featT = work.tile([P, GROUP], BF16, name="featT")
-                nc.scalar.copy(out=featT[:], in_=feat_ps[:])
-                return codes, scales, featT
-
-            def multiply(g, s, operands):
-                codes, scales, featT = operands
-                kind = min(s, 1)
-                w_codes, w_scales = lin_w[kind]
-                bypass = []
-                for h in range(HALVES):
-                    chans = slice(h * P, (h + 1) * P)
-                    byp_ps = psum_byp.tile([P, GROUP], F32, name="byp_ps")
-                    nc.tensor.matmul(
-                        out=byp_ps[:], lhsT=byp_w[kind][:, chans], rhs=featT[:], start=True, stop=True
-                    )
-                    byp_sb = work.tile([P, GROUP], F32, name="byp_sb")
-                    nc.scalar.mul(out=byp_sb[:], in_=byp_ps[:], mul=1.0 / math.sqrt(INP))
-                    bypass.append(byp_sb)
-                for h in range(HALVES):
-                    chans = slice(h * P, (h + 1) * P)
-                    mx_ps = psum_mx.tile([P, GROUP], F32, name="mx_ps")
-                    nc.tensor.matmul_mx(
-                        out=mx_ps[:],
-                        lhsT=w_codes[:, chans].bitcast(FP8X4),
-                        lhsT_scale=w_scales[:, chans],
-                        rhs=codes[:].bitcast(FP8X4),
-                        rhs_scale=scales[:],
-                        start=True,
-                        stop=True,
-                    )
-                    nc.vector.scalar_tensor_tensor(
-                        out=y[g][:, h, s, :],
-                        in0=mx_ps[:],
-                        scalar=1.0 / math.sqrt(HID),
-                        in1=bypass[h][:],
-                        op0=ALU.mult,
-                        op1=ALU.add,
-                    )
-                for h in range(HALVES):
-                    if s == 0:
-                        chunk = stats_scal[:, h, g, :]
-                    else:
-                        chunk = stats_vec[:, h, g * DV + s - 1, :]
-                    nc.vector.bn_stats(out=chunk, in_=y[g][:, h, s, :])
-
-            todo = [(g, s) for g in range(GROUPS) for s in range(SECTIONS)]
-            load(0)
-            load(1)
-            ready = prepare(*todo[0])
-            for i in range(1, len(todo)):
+            load_scal(0)
+            load_vec(0, vec_in)
+            load_vec(1, vec_in)
+            ready = prepare(*todo[0], banks_a, vec_in)
+            for i in range(1, first_late):
                 g, s = todo[i]
-                if s == 0 and g + 1 < GROUPS:
-                    load(g + 1)
-                following = prepare(g, s)
-                multiply(todo[i - 1][0], todo[i - 1][1], ready)
+                if s == 1 and g + 2 < GROUPS:
+                    load_vec(g + 2, vec_in)
+                    if g % 2 == 0 and 0 < g // 2 + 1 < EARLY:
+                        load_scal(g // 2 + 1)
+                following = prepare(g, s, banks_a, vec_in)
+                multiply(*todo[i - 1], ready, banks_a)
                 ready = following
-            multiply(todo[-1][0], todo[-1][1], ready)
+            load_scal(EARLY)
+            load_scal(EARLY + 1)
+            multiply(*todo[first_late - 1], ready, banks_a)
 
-        moments = consts.tile([P, 2 * HALVES, 2], F32)
-        for h in range(HALVES):
-            nc.vector.bn_aggr(
-                out=moments[:, h, :], in_=stats_scal[:, h].rearrange("p c s -> p (c s)")
+        with ExitStack() as part_b:
+            rows_pool = part_b.enter_context(tc.tile_pool(name="rows", bufs=4))
+            banks_b = {
+                "x": part_b.enter_context(tc.psum_pool(name="psum_xb", bufs=2)),
+                "f": part_b.enter_context(tc.psum_pool(name="psum_fb", bufs=1)),
+                "mx": part_b.enter_context(tc.psum_pool(name="psum_mxb", bufs=1)),
+                "byp": part_b.enter_context(tc.psum_pool(name="psum_bypb", bufs=1)),
+            }
+            psum_out = part_b.enter_context(tc.psum_pool(name="psum_out", bufs=3))
+
+            scale_vec = norm_scale(stats_vec, 1)[1]
+            scale_ps = psum_out.tile([P, P], F32, tag="vec_ps")
+            nc.tensor.matmul(
+                out=scale_ps[:],
+                lhsT=scale_vec[:, 0:1].to_broadcast([P, P]),
+                rhs=ident_f32[:],
+                start=True,
+                stop=True,
             )
-            nc.vector.bn_aggr(
-                out=moments[:, HALVES + h, :], in_=stats_vec[:, h].rearrange("p c s -> p (c s)")
-            )
-        mean_sq = consts.tile([P, HALVES], F32)
-        nc.vector.tensor_mul(out=mean_sq[:], in0=moments[:, HALVES:, 0], in1=moments[:, HALVES:, 0])
-        spread = consts.tile([P, 2 * HALVES], F32)
-        nc.vector.tensor_scalar_add(out=spread[:, 0:HALVES], in0=moments[:, 0:HALVES, 1], scalar1=EPS)
-        nc.vector.scalar_tensor_tensor(
-            out=spread[:, HALVES:],
-            in0=moments[:, HALVES:, 1],
-            scalar=EPS,
-            in1=mean_sq[:],
-            op0=ALU.add,
-            op1=ALU.add,
-        )
-        root = consts.tile([P, 2 * HALVES], F32)
-        nc.scalar.sqrt(out=root[:], in_=spread[:])
-        scale = consts.tile([P, 2 * HALVES], F32)
-        nc.vector.reciprocal(out=scale[:], in_=root[:])
-        nc.vector.tensor_mul(out=scale[:], in0=scale[:], in1=bn_cols[:, 0 : 2 * HALVES])
-        shift = consts.tile([P, 2 * HALVES], F32)
-        nc.vector.memset(shift[:], 0.0)
-        scaled_mean = consts.tile([P, HALVES], F32)
-        nc.vector.tensor_mul(out=scaled_mean[:], in0=moments[:, 0:HALVES, 0], in1=scale[:, 0:HALVES])
-        nc.vector.tensor_sub(
-            out=shift[:, 0:HALVES], in0=bn_cols[:, 2 * HALVES : 3 * HALVES], in1=scaled_mean[:]
-        )
+            scale_row = consts.tile([P, P], F32)
+            nc.vector.tensor_copy(out=scale_row[:], in_=scale_ps[:])
 
-        with ExitStack() as phase2:
-            rows_pool = phase2.enter_context(tc.tile_pool(name="rows", bufs=3))
-            psum_s = phase2.enter_context(tc.psum_pool(name="psum_s", bufs=2))
-            psum_v = phase2.enter_context(tc.psum_pool(name="psum_v", bufs=6))
-
-            def normalise(g):
-                for h in range(HALVES):
-                    nc.scalar.activation(
-                        out=y[g][:, h, 0, :],
-                        in_=y[g][:, h, 0, :],
-                        func=ACT.Identity,
-                        scale=scale[:, h : h + 1],
-                        bias=shift[:, h : h + 1],
-                    )
-                    b = HALVES + h
-                    nc.gpsimd.tensor_scalar(
-                        out=y[g][:, h, 1:, :],
-                        in0=y[g][:, h, 1:, :],
-                        scalar1=scale[:, b : b + 1],
-                        scalar2=shift[:, b : b + 1],
-                        op0=ALU.mult,
-                        op1=ALU.add,
-                    )
-
-            def store(g, half):
-                rows_sb = rows_pool.tile([P, 2, SECTIONS * OUTC], F32, name="rows_sb")
-                scal_ps = psum_s.tile([P, 2, HALVES, P], F32, name="scal_ps")
-                for jj in range(2):
-                    nodes = slice((2 * half + jj) * P, (2 * half + jj + 1) * P)
-                    for h in range(HALVES):
-                        nc.tensor.transpose(scal_ps[:, jj, h, :], y[g][:, h, 0, nodes], ident_f32[:])
-                nc.vector.tensor_copy(
-                    out=rows_sb[:, :, 0:OUTC], in_=scal_ps[:].rearrange("p j h c -> p j (h c)")
+            def prescale(g, half):
+                nodes = slice(half * GROUP // 2, (half + 1) * GROUP // 2)
+                nc.gpsimd.tensor_scalar(
+                    out=y_vec[g][:, 1, :, nodes],
+                    in0=y_vec[g][:, 1, :, nodes],
+                    scalar1=scale_vec[:, 1:2],
+                    scalar2=0.0,
+                    op0=ALU.mult,
+                    op1=ALU.add,
                 )
+
+            def store_vec(g, half):
+                rows_sb = rows_pool.tile([P, 2, DV * OUTC], F32, name="rows_vec")
                 for jj in range(2):
                     nodes = slice((2 * half + jj) * P, (2 * half + jj + 1) * P)
                     for h in range(HALVES):
-                        vec_ps = psum_v.tile([P, DV, P], F32, name="vec_ps")
+                        vec_ps = psum_out.tile([P, DV, P], F32, name="vec_ps")
                         for d in range(DV):
-                            nc.tensor.transpose(vec_ps[:, d, :], y[g][:, h, 1 + d, nodes], ident_f32[:])
-                        first = OUTC + h * DV * P
-                        dest = rows_sb[:, jj, first : first + DV * P].rearrange("p (o d) -> p o d", d=DV)
+                            nc.tensor.transpose(vec_ps[:, d, :], y_vec[g][:, h, d, nodes], ident_f32[:])
+                        dest = rows_sb[:, jj, h * DV * P : (h + 1) * DV * P].rearrange(
+                            "p (o d) -> p o d", d=DV
+                        )
                         if h == 0:
-                            nc.vector.tensor_copy(out=dest, in_=vec_ps[:].rearrange("p d o -> p o d"))
+                            nc.vector.tensor_tensor(
+                                out=dest,
+                                in0=vec_ps[:].rearrange("p d o -> p o d"),
+                                in1=scale_row[:].unsqueeze(2).to_broadcast([P, P, DV]),
+                                op=ALU.mult,
+                            )
                         else:
                             nc.scalar.copy(out=dest, in_=vec_ps[:].rearrange("p d o -> p o d"))
-                group_rows = out[g * GROUP : (g + 1) * GROUP, :].rearrange("(p j) c -> p j c", j=J)
+                group_rows = out[g * GROUP : (g + 1) * GROUP, OUTC:].rearrange("(p j) c -> p j c", j=J)
                 nc.sync.dma_start(out=group_rows[:, 2 * half : 2 * half + 2, :], in_=rows_sb[:])
 
-            normalise(0)
+            stores = [(g, half) for g in range(GROUPS) for half in range(2)]
+            late = len(todo) - first_late
+            prescale(*stores[0])
+            prescale(*stores[1])
+            done = 0
+            ready = None
+            for i in range(late + 1):
+                following = None
+                if i < late:
+                    g = todo[first_late + i][0]
+                    if i >= 1 and g + 1 < GROUPS:
+                        load_scal(g + 1)
+                    following = prepare(*todo[first_late + i], banks_b, None)
+                if ready is not None:
+                    multiply(*todo[first_late + i - 1], ready, banks_b)
+                ready = following
+                until = len(stores) * (i + 1) // (late + 1)
+                while done < until:
+                    if done + 2 < len(stores):
+                        prescale(*stores[done + 2])
+                    store_vec(*stores[done])
+                    done += 1
+
+            moments, scale_scal = norm_scale(stats_scal, 0)
+            scaled_mean = consts.tile([P, HALVES], F32)
+            nc.vector.tensor_mul(out=scaled_mean[:], in0=moments[:, :, 0], in1=scale_scal[:])
+            shift = consts.tile([P, HALVES], F32)
+            nc.vector.tensor_sub(
+                out=shift[:], in0=bn_cols[:, 2 * HALVES : 3 * HALVES], in1=scaled_mean[:]
+            )
             for g in range(GROUPS):
-                if g + 1 < GROUPS:
-                    normalise(g + 1)
+                for h in range(HALVES):
+                    if h == 0:
+                        nc.scalar.activation(
+                            out=y_scal[g][:, h, :],
+                            in_=y_scal[g][:, h, :],
+                            func=ACT.Identity,
+                            scale=scale_scal[:, h : h + 1],
+                            bias=shift[:, h : h + 1],
+                        )
+                    else:
+                        nc.vector.tensor_scalar(
+                            out=y_scal[g][:, h, :],
+                            in0=y_scal[g][:, h, :],
+                            scalar1=scale_scal[:, h : h + 1],
+                            scalar2=shift[:, h : h + 1],
+                            op0=ALU.mult,
+                            op1=ALU.add,
+                        )
+                rows_sb = rows_pool.tile([P, J, OUTC], F32, name="rows_scal", bufs=3)
                 for half in range(2):
-                    store(g, half)
+                    scal_ps = psum_out.tile([P, 2, HALVES, P], F32, tag="vec_ps")
+                    for jj in range(2):
+                        nodes = slice((2 * half + jj) * P, (2 * half + jj + 1) * P)
+                        for h in range(HALVES):
+                            nc.tensor.transpose(scal_ps[:, jj, h, :], y_scal[g][:, h, nodes], ident_f32[:])
+                    dest = rows_sb[:, 2 * half : 2 * half + 2, :]
+                    flat = scal_ps[:].rearrange("p j h c -> p j (h c)")
+                    if half == 0:
+                        nc.scalar.copy(out=dest, in_=flat)
+                    else:
+                        nc.vector.tensor_copy(out=dest, in_=flat)
+                group_rows = out[g * GROUP : (g + 1) * GROUP, 0:OUTC].rearrange("(p j) c -> p j c", j=J)
+                nc.sync.dma_start(out=group_rows, in_=rows_sb[:])

@@ -25,15 +25,15 @@ J = GROUP // P
 GROUPS = NODES // GROUP
 STATS = 6
 EPS = 1e-5
-EARLY = 4
+EARLY = 2
 
 FLOPS = 2 * NODES * SECTIONS * OUTC * (HID + INP)
 
 
 def quantise_weight(nc, pool, w, label):
-    raw = pool.tile([P, 4, OUTC], BF16, name="w_raw")
-    nc.scalar.dma_start(out=raw[:], in_=w.rearrange("(p t) c -> p t c", t=4))
-    grouped = pool.tile([P, OUTC, 4], BF16, name="w_grouped", align_bytes=64)
+    raw = pool.tile([P, 4, OUTC], BF16, name="w_raw", bufs=2)
+    nc.sync.dma_start(out=raw[:], in_=w.rearrange("(p t) c -> p t c", t=4))
+    grouped = pool.tile([P, OUTC, 4], BF16, name="w_grouped", align_bytes=64, bufs=2)
     nc.vector.tensor_copy(out=grouped[:], in_=raw[:].rearrange("p t c -> p c t"))
     codes = pool.tile([P, OUTC], U32, name=label + "_codes", align_bytes=64)
     scales = pool.tile([P, OUTC], U8, name=label + "_scales", align_bytes=64)
@@ -64,26 +64,26 @@ def tile_feedforward_pb_t_kernel(
         nc.vector.memset(warm[:], 1.0)
         nc.scalar.sqrt(out=warm[:], in_=warm[:])
 
-        lin_w = [
-            quantise_weight(nc, consts, lin3_W0, "w0"),
-            quantise_weight(nc, consts, lin3_W1, "w1"),
-        ]
-        byp_w = []
-        for label, w in (("byp0", byp_W0), ("byp1", byp_W1)):
-            w_sb = consts.tile([P, OUTC], BF16, name=label)
-            nc.scalar.dma_start(out=w_sb[:], in_=w)
-            byp_w.append(w_sb)
+        lin_w = {}
+        byp_w = {}
+
+        def load_weights(kind, w_hidden, w_bypass):
+            lin_w[kind] = quantise_weight(nc, consts, w_hidden, "w%d" % kind)
+            byp_w[kind] = consts.tile([P, OUTC], BF16, name="byp%d" % kind)
+            nc.sync.dma_start(out=byp_w[kind][:], in_=w_bypass)
 
         bn_rows = consts.tile([P, P], BF16)
         nc.vector.memset(bn_rows[:], 0.0)
-        nc.scalar.dma_start(out=bn_rows[0:4, :], in_=bn_weight.rearrange("(r c) -> r c", c=P))
-        nc.scalar.dma_start(out=bn_rows[4:6, :], in_=bn_bias.rearrange("(r c) -> r c", c=P))
         bn_cols = consts.tile([P, 6], F32)
 
         y_scal = [y_pool.tile([P, HALVES, GROUP], F32, name="ys%d" % g) for g in range(GROUPS)]
         y_vec = [y_pool.tile([P, HALVES, DV, GROUP], F32, name="yv%d" % g) for g in range(GROUPS)]
         stats_scal = consts.tile([P, HALVES, GROUPS, STATS], F32)
-        stats_vec = consts.tile([P, HALVES, GROUPS * DV, STATS], F32)
+        stats_vec = [
+            consts.tile([P, GROUPS * DV, STATS], F32, name="stats_vec0"),
+            consts.tile([P, GROUPS * (DV - 1), STATS], F32, name="stats_vec1"),
+        ]
+        squares = consts.tile([P, GROUPS], F32)
 
         loaded = {}
 
@@ -193,15 +193,27 @@ def tile_feedforward_pb_t_kernel(
             for h in range(HALVES):
                 if s == 0:
                     nc.vector.bn_stats(out=stats_scal[:, h, g, :], in_=y_scal[g][:, h, :])
-                else:
+                elif h == 0:
                     nc.vector.bn_stats(
-                        out=stats_vec[:, h, g * DV + s - 1, :], in_=y_vec[g][:, h, s - 1, :]
+                        out=stats_vec[0][:, g * DV + s - 1, :], in_=y_vec[g][:, h, s - 1, :]
+                    )
+                elif s < DV:
+                    nc.vector.bn_stats(
+                        out=stats_vec[1][:, g * (DV - 1) + s - 1, :], in_=y_vec[g][:, h, s - 1, :]
+                    )
+                else:
+                    squared = work.tile([P, GROUP], BF16, name="squared")
+                    nc.scalar.activation(
+                        out=squared[:],
+                        in_=y_vec[g][:, h, s - 1, :],
+                        func=ACT.Square,
+                        accum_out=squares[:, g : g + 1],
                     )
 
         def norm_scale(stats, kind):
             moments = consts.tile([P, HALVES, 2], F32, name="moments%d" % kind)
             for h in range(HALVES):
-                nc.vector.bn_aggr(out=moments[:, h, :], in_=stats[:, h].rearrange("p c s -> p (c s)"))
+                nc.vector.bn_aggr(out=moments[:, h, :], in_=stats[h].rearrange("p c s -> p (c s)"))
             spread = consts.tile([P, HALVES], F32, name="spread%d" % kind)
             if kind == 0:
                 nc.vector.tensor_scalar_add(out=spread[:], in0=moments[:, :, 1], scalar1=EPS)
@@ -216,6 +228,25 @@ def tile_feedforward_pb_t_kernel(
                     op0=ALU.add,
                     op1=ALU.add,
                 )
+                total = consts.tile([P, 1], F32)
+                nc.vector.reduce_sum(out=total[:], in_=squares[:], axis=mybir.AxisListType.X)
+                rest = consts.tile([P, 1], F32)
+                nc.vector.tensor_scalar(
+                    out=rest[:],
+                    in0=total[:],
+                    scalar1=1.0 / (NODES * DV),
+                    scalar2=EPS / DV,
+                    op0=ALU.mult,
+                    op1=ALU.add,
+                )
+                nc.vector.scalar_tensor_tensor(
+                    out=spread[:, 1:2],
+                    in0=spread[:, 1:2],
+                    scalar=(DV - 1) / DV,
+                    in1=rest[:],
+                    op0=ALU.mult,
+                    op1=ALU.add,
+                )
             root = consts.tile([P, HALVES], F32, name="root%d" % kind)
             nc.scalar.sqrt(out=root[:], in_=spread[:])
             inverse = consts.tile([P, HALVES], F32, name="inverse%d" % kind)
@@ -226,10 +257,8 @@ def tile_feedforward_pb_t_kernel(
             )
             return moments, scale
 
-        todo = []
+        todo = [(g, 0) for g in range(EARLY)]
         for g in range(GROUPS):
-            if g % 2 == 0 and g // 2 < EARLY:
-                todo.append((g // 2, 0))
             todo += [(g, s) for s in range(1, SECTIONS)]
         first_late = len(todo)
         todo += [(g, 0) for g in range(EARLY, GROUPS)]
@@ -242,20 +271,19 @@ def tile_feedforward_pb_t_kernel(
                 "mx": part_a.enter_context(tc.psum_pool(name="psum_mxa", bufs=2)),
                 "byp": part_a.enter_context(tc.psum_pool(name="psum_bypa", bufs=2)),
             }
-            bn_ps = banks_a["f"].tile([P, P], BF16, tag="feat_ps")
-            nc.tensor.transpose(bn_ps[:], bn_rows[:], ident_bf16[:])
-            nc.vector.tensor_copy(out=bn_cols[:], in_=bn_ps[:, 0:6])
-
             load_scal(0)
+            load_weights(0, lin3_W0, byp_W0)
+            load_scal(1)
             load_vec(0, vec_in)
+            load_weights(1, lin3_W1, byp_W1)
             load_vec(1, vec_in)
+            nc.sync.dma_start(out=bn_rows[0:4, :], in_=bn_weight.rearrange("(r c) -> r c", c=P))
+            nc.sync.dma_start(out=bn_rows[4:6, :], in_=bn_bias.rearrange("(r c) -> r c", c=P))
             ready = prepare(*todo[0], banks_a, vec_in)
             for i in range(1, first_late):
                 g, s = todo[i]
                 if s == 1 and g + 2 < GROUPS:
                     load_vec(g + 2, vec_in)
-                    if g % 2 == 0 and 0 < g // 2 + 1 < EARLY:
-                        load_scal(g // 2 + 1)
                 following = prepare(g, s, banks_a, vec_in)
                 multiply(*todo[i - 1], ready, banks_a)
                 ready = following
@@ -273,7 +301,11 @@ def tile_feedforward_pb_t_kernel(
             }
             psum_out = part_b.enter_context(tc.psum_pool(name="psum_out", bufs=3))
 
-            scale_vec = norm_scale(stats_vec, 1)[1]
+            bn_ps = banks_b["f"].tile([P, P], BF16, tag="feat_ps")
+            nc.tensor.transpose(bn_ps[:], bn_rows[:], ident_bf16[:])
+            nc.vector.tensor_copy(out=bn_cols[:], in_=bn_ps[:, 0:6])
+
+            scale_vec = norm_scale([stats_vec[0][:], stats_vec[1][:]], 1)[1]
             scale_ps = psum_out.tile([P, P], F32, tag="vec_ps")
             nc.tensor.matmul(
                 out=scale_ps[:],
@@ -342,7 +374,7 @@ def tile_feedforward_pb_t_kernel(
                     store_vec(*stores[done])
                     done += 1
 
-            moments, scale_scal = norm_scale(stats_scal, 0)
+            moments, scale_scal = norm_scale([stats_scal[:, 0], stats_scal[:, 1]], 0)
             scaled_mean = consts.tile([P, HALVES], F32)
             nc.vector.tensor_mul(out=scaled_mean[:], in0=moments[:, :, 0], in1=scale_scal[:])
             shift = consts.tile([P, HALVES], F32)

@@ -25,7 +25,7 @@ J = GROUP // P
 GROUPS = NODES // GROUP
 STATS = 6
 EPS = 1e-5
-EARLY = 2
+EARLY = 4
 
 FLOPS = 2 * NODES * SECTIONS * OUTC * (HID + INP)
 
@@ -79,11 +79,7 @@ def tile_feedforward_pb_t_kernel(
         y_scal = [y_pool.tile([P, HALVES, GROUP], F32, name="ys%d" % g) for g in range(GROUPS)]
         y_vec = [y_pool.tile([P, HALVES, DV, GROUP], F32, name="yv%d" % g) for g in range(GROUPS)]
         stats_scal = consts.tile([P, HALVES, GROUPS, STATS], F32)
-        stats_vec = [
-            consts.tile([P, GROUPS * DV, STATS], F32, name="stats_vec0"),
-            consts.tile([P, GROUPS * (DV - 1), STATS], F32, name="stats_vec1"),
-        ]
-        squares = consts.tile([P, GROUPS], F32)
+        stats_vec = consts.tile([P, HALVES, GROUPS * DV, STATS], F32)
 
         loaded = {}
 
@@ -193,21 +189,9 @@ def tile_feedforward_pb_t_kernel(
             for h in range(HALVES):
                 if s == 0:
                     nc.vector.bn_stats(out=stats_scal[:, h, g, :], in_=y_scal[g][:, h, :])
-                elif h == 0:
-                    nc.vector.bn_stats(
-                        out=stats_vec[0][:, g * DV + s - 1, :], in_=y_vec[g][:, h, s - 1, :]
-                    )
-                elif s < DV:
-                    nc.vector.bn_stats(
-                        out=stats_vec[1][:, g * (DV - 1) + s - 1, :], in_=y_vec[g][:, h, s - 1, :]
-                    )
                 else:
-                    squared = work.tile([P, GROUP], BF16, name="squared")
-                    nc.scalar.activation(
-                        out=squared[:],
-                        in_=y_vec[g][:, h, s - 1, :],
-                        func=ACT.Square,
-                        accum_out=squares[:, g : g + 1],
+                    nc.vector.bn_stats(
+                        out=stats_vec[:, h, g * DV + s - 1, :], in_=y_vec[g][:, h, s - 1, :]
                     )
 
         def norm_scale(stats, kind):
@@ -228,25 +212,6 @@ def tile_feedforward_pb_t_kernel(
                     op0=ALU.add,
                     op1=ALU.add,
                 )
-                total = consts.tile([P, 1], F32)
-                nc.vector.reduce_sum(out=total[:], in_=squares[:], axis=mybir.AxisListType.X)
-                rest = consts.tile([P, 1], F32)
-                nc.vector.tensor_scalar(
-                    out=rest[:],
-                    in0=total[:],
-                    scalar1=1.0 / (NODES * DV),
-                    scalar2=EPS / DV,
-                    op0=ALU.mult,
-                    op1=ALU.add,
-                )
-                nc.vector.scalar_tensor_tensor(
-                    out=spread[:, 1:2],
-                    in0=spread[:, 1:2],
-                    scalar=(DV - 1) / DV,
-                    in1=rest[:],
-                    op0=ALU.mult,
-                    op1=ALU.add,
-                )
             root = consts.tile([P, HALVES], F32, name="root%d" % kind)
             nc.scalar.sqrt(out=root[:], in_=spread[:])
             inverse = consts.tile([P, HALVES], F32, name="inverse%d" % kind)
@@ -257,8 +222,10 @@ def tile_feedforward_pb_t_kernel(
             )
             return moments, scale
 
-        todo = [(g, 0) for g in range(EARLY)]
+        todo = [(0, 0), (1, 0)]
         for g in range(GROUPS):
+            if g % 2 == 1 and 2 + g // 2 < EARLY:
+                todo.append((2 + g // 2, 0))
             todo += [(g, s) for s in range(1, SECTIONS)]
         first_late = len(todo)
         todo += [(g, 0) for g in range(EARLY, GROUPS)]
@@ -284,6 +251,8 @@ def tile_feedforward_pb_t_kernel(
                 g, s = todo[i]
                 if s == 1 and g + 2 < GROUPS:
                     load_vec(g + 2, vec_in)
+                    if g % 2 == 0 and 2 + g // 2 < EARLY:
+                        load_scal(2 + g // 2)
                 following = prepare(g, s, banks_a, vec_in)
                 multiply(*todo[i - 1], ready, banks_a)
                 ready = following
@@ -305,7 +274,7 @@ def tile_feedforward_pb_t_kernel(
             nc.tensor.transpose(bn_ps[:], bn_rows[:], ident_bf16[:])
             nc.vector.tensor_copy(out=bn_cols[:], in_=bn_ps[:, 0:6])
 
-            scale_vec = norm_scale([stats_vec[0][:], stats_vec[1][:]], 1)[1]
+            scale_vec = norm_scale([stats_vec[:, 0], stats_vec[:, 1]], 1)[1]
             scale_ps = psum_out.tile([P, P], F32, tag="vec_ps")
             nc.tensor.matmul(
                 out=scale_ps[:],

@@ -25,14 +25,18 @@ J = GROUP // P
 GROUPS = NODES // GROUP
 STATS = 6
 EPS = 1e-5
-EARLY = 4
+EPS_HID = EPS * HID
+SORT_AHEAD = 5
+STATS_BEHIND = 5
+BEHIND = (1, 3)
+LATE = 4
+LATE_STEP = 2
+SQUARED = (3,)
 
 FLOPS = 2 * NODES * SECTIONS * OUTC * (HID + INP)
 
 
-def quantise_weight(nc, pool, w, label):
-    raw = pool.tile([P, 4, OUTC], BF16, name="w_raw", bufs=2)
-    nc.sync.dma_start(out=raw[:], in_=w.rearrange("(p t) c -> p t c", t=4))
+def quantise_weight(nc, pool, raw, label):
     grouped = pool.tile([P, OUTC, 4], BF16, name="w_grouped", align_bytes=64, bufs=2)
     nc.vector.tensor_copy(out=grouped[:], in_=raw[:].rearrange("p t c -> p c t"))
     codes = pool.tile([P, OUTC], U32, name=label + "_codes", align_bytes=64)
@@ -68,9 +72,11 @@ def tile_feedforward_pb_t_kernel(
         byp_w = {}
 
         def load_weights(kind, w_hidden, w_bypass):
-            lin_w[kind] = quantise_weight(nc, consts, w_hidden, "w%d" % kind)
+            raw = consts.tile([P, 4, OUTC], BF16, name="w_raw", bufs=2)
+            nc.scalar.dma_start(out=raw[:], in_=w_hidden.rearrange("(p t) c -> p t c", t=4))
+            lin_w[kind] = quantise_weight(nc, consts, raw, "w%d" % kind)
             byp_w[kind] = consts.tile([P, OUTC], BF16, name="byp%d" % kind)
-            nc.sync.dma_start(out=byp_w[kind][:], in_=w_bypass)
+            nc.scalar.dma_start(out=byp_w[kind][:], in_=w_bypass)
 
         bn_rows = consts.tile([P, P], BF16)
         nc.vector.memset(bn_rows[:], 0.0)
@@ -78,10 +84,22 @@ def tile_feedforward_pb_t_kernel(
 
         y_scal = [y_pool.tile([P, HALVES, GROUP], F32, name="ys%d" % g) for g in range(GROUPS)]
         y_vec = [y_pool.tile([P, HALVES, DV, GROUP], F32, name="yv%d" % g) for g in range(GROUPS)]
+        own = DV - len(SQUARED)
         stats_scal = consts.tile([P, HALVES, GROUPS, STATS], F32)
-        stats_vec = consts.tile([P, HALVES, GROUPS * DV, STATS], F32)
+        stats_vec = [
+            consts.tile([P, GROUPS * DV, STATS], F32, name="stats_vec0"),
+            consts.tile([P, GROUPS * own, STATS], F32, name="stats_vec1"),
+        ]
+        squares = consts.tile([P, GROUPS * len(SQUARED)], F32)
 
-        loaded = {}
+        hidden_of = {}
+        feat_of = {}
+        sorted_comp = {}
+        grouped_of = {}
+        operands = {}
+        featT_of = {}
+        bypass_of = {}
+        mx_of = {}
 
         def load_scal(g):
             rows = slice(g * GROUP, (g + 1) * GROUP)
@@ -93,189 +111,242 @@ def tile_feedforward_pb_t_kernel(
             nc.sync.dma_start(
                 out=feat[:], in_=features[rows, 0:INP].rearrange("(p j) k -> p j k", j=J)
             )
-            loaded[(g, 0)] = (hidden, feat)
+            hidden_of[(g, 0)] = hidden
+            feat_of[(g, 0)] = feat
 
-        def load_vec(g, vec_in):
-            rows = slice(g * GROUP, (g + 1) * GROUP)
-            hidden = vec_in.tile([P, J, DV * HID], BF16, name="h2_vec")
-            nc.sync.dma_start(
-                out=hidden[:], in_=h2[rows, HID:].rearrange("(p j) k -> p j k", j=J)
-            )
+        def load_hidden(g, vec_in):
+            rows = h2[g * GROUP : (g + 1) * GROUP, HID:].rearrange("(p j) k -> p j k", j=J)
+            hidden = vec_in.tile([P, J, DV * HID], BF16, name="h2_vec", bufs=2)
+            nc.sync.dma_start(out=hidden[:], in_=rows)
+            hidden_of.update({(g, s): hidden for s in range(1, SECTIONS)})
+
+        def load_feat(g, vec_in):
+            rows = features[g * GROUP : (g + 1) * GROUP, INP:].rearrange("(p j) k -> p j k", j=J)
             feat = vec_in.tile([P, J, DV * INP], BF16, name="feat_vec")
-            nc.sync.dma_start(
-                out=feat[:], in_=features[rows, INP:].rearrange("(p j) k -> p j k", j=J)
-            )
-            for s in range(1, SECTIONS):
-                loaded[(g, s)] = (hidden, feat)
+            nc.sync.dma_start(out=feat[:], in_=rows)
+            feat_of.update({(g, s): feat for s in range(1, SECTIONS)})
 
-        def prepare(g, s, banks, vec_in):
-            source, feat = loaded[(g, s)]
-            hidden = source if s == 0 else vec_in.tile([P, J, HID], BF16, name="h2_comp")
-            grouped = work.tile([P, GROUP, 2], F32, name="grouped", align_bytes=64)
+        def sort(g, s, vec_in):
+            comp = vec_in.tile([P, J, HID], BF16, name="h2_comp")
             for half in range(2):
-                hid_ps = banks["x"].tile([P, 2, 2 * P], F32, name="hid_ps")
-                if s > 0:
-                    pair = slice(2 * half, 2 * half + 2)
-                    nc.gpsimd.tensor_scalar(
-                        out=hidden[:, pair, :],
-                        in0=source[:, pair, :].rearrange("p j (i d) -> p d j i", d=DV)[:, s - 1],
-                        scalar1=1.0,
-                        scalar2=0.0,
-                        op0=ALU.mult,
-                        op1=ALU.add,
-                    )
-                for jj in range(2):
-                    words = hidden[:, 2 * half + jj, :].bitcast(F32)
-                    for u in range(2):
-                        nc.tensor.transpose(
-                            hid_ps[:, u, jj * P : (jj + 1) * P], words[:, u::2], ident_f32[:]
-                        )
-                nc.scalar.copy(
-                    out=grouped[:, half * 2 * P : (half + 1) * 2 * P, :],
-                    in_=hid_ps[:].rearrange("p u n -> p n u"),
+                pair = slice(2 * half, 2 * half + 2)
+                nc.gpsimd.tensor_scalar(
+                    out=comp[:, pair, :],
+                    in0=hidden_of[(g, s)][:, pair, :].rearrange("p j (i d) -> p d j i", d=DV)[:, s - 1],
+                    scalar1=1.0,
+                    scalar2=0.0,
+                    op0=ALU.mult,
+                    op1=ALU.add,
                 )
-            codes = work.tile([P, GROUP], U32, name="codes", align_bytes=64)
-            scales = work.tile([P, GROUP], U8, name="scales", align_bytes=64)
+            sorted_comp[(g, s)] = comp
+
+        def turn(g, s, half, banks):
+            if half == 0:
+                grouped_of[(g, s)] = work.tile([P, GROUP, 4], BF16, name="grouped", align_bytes=64)
+            dest = grouped_of[(g, s)][:, half * 2 * P : (half + 1) * 2 * P, :]
+            hidden = hidden_of[(g, s)] if s == 0 else sorted_comp[(g, s)]
+            hid_ps = banks["x"].tile([P, 2, 2 * P], F32, name="hid_ps")
+            for jj in range(2):
+                words = hidden[:, 2 * half + jj, :].bitcast(F32)
+                for u in range(2):
+                    nc.tensor.transpose(
+                        hid_ps[:, u, jj * P : (jj + 1) * P], words[:, u::2], ident_f32[:]
+                    )
+            nc.scalar.copy(
+                out=dest.rearrange("p n t -> p (n t)").bitcast(F32).rearrange("p (n u) -> p n u", u=2),
+                in_=hid_ps[:].rearrange("p u n -> p n u"),
+            )
+
+        def quantise(g, s):
+            codes = work.tile([P, GROUP], U32, name="codes", align_bytes=64, bufs=3)
+            scales = work.tile([P, GROUP], U8, name="scales", align_bytes=64, bufs=3)
             nc.vector.quantize_mx(
                 out=codes[:].bitcast(FP8X4),
                 scales=scales[:],
-                in_=grouped[:].rearrange("p n w -> p (n w)").bitcast(BF16),
+                in_=grouped_of[(g, s)][:].rearrange("p n t -> p (n t)"),
             )
+            operands[(g, s)] = (codes, scales)
+
+        def turn_bypass(g, s, banks):
+            feat = feat_of[(g, s)]
             feat_ps = banks["f"].tile([P, GROUP], BF16, name="feat_ps")
             for j in range(J):
                 cols = feat[:, j, :]
                 if s > 0:
                     cols = cols.rearrange("p (i d) -> p d i", d=DV)[:, s - 1]
                 nc.tensor.transpose(feat_ps[:, j * P : (j + 1) * P], cols, ident_bf16[:])
-            featT = work.tile([P, GROUP], BF16, name="featT", bufs=3)
+            featT = work.tile([P, GROUP], BF16, name="featT", bufs=4)
             nc.scalar.copy(out=featT[:], in_=feat_ps[:])
-            return codes, scales, featT
+            featT_of[(g, s)] = featT
 
-        def multiply(g, s, operands, banks):
-            codes, scales, featT = operands
-            kind = min(s, 1)
-            w_codes, w_scales = lin_w[kind]
-            bypass = []
-            for h in range(HALVES):
-                chans = slice(h * P, (h + 1) * P)
-                byp_ps = banks["byp"].tile([P, GROUP], F32, name="byp_ps")
-                nc.tensor.matmul(
-                    out=byp_ps[:], lhsT=byp_w[kind][:, chans], rhs=featT[:], start=True, stop=True
-                )
-                byp_sb = work.tile([P, GROUP], F32, name="byp_sb", bufs=4)
-                nc.scalar.mul(out=byp_sb[:], in_=byp_ps[:], mul=1.0 / math.sqrt(INP))
-                bypass.append(byp_sb)
-            for h in range(HALVES):
-                chans = slice(h * P, (h + 1) * P)
-                mx_ps = banks["mx"].tile([P, GROUP], F32, name="mx_ps")
-                nc.tensor.matmul_mx(
-                    out=mx_ps[:],
-                    lhsT=w_codes[:, chans].bitcast(FP8X4),
-                    lhsT_scale=w_scales[:, chans],
-                    rhs=codes[:].bitcast(FP8X4),
-                    rhs_scale=scales[:],
-                    start=True,
-                    stop=True,
-                )
-                y = y_scal[g][:, h, :] if s == 0 else y_vec[g][:, h, s - 1, :]
-                nc.vector.scalar_tensor_tensor(
-                    out=y,
-                    in0=mx_ps[:],
-                    scalar=1.0 / math.sqrt(HID),
-                    in1=bypass[h][:],
-                    op0=ALU.mult,
-                    op1=ALU.add,
-                )
-            for h in range(HALVES):
-                if s == 0:
-                    nc.vector.bn_stats(out=stats_scal[:, h, g, :], in_=y_scal[g][:, h, :])
-                else:
-                    nc.vector.bn_stats(
-                        out=stats_vec[:, h, g * DV + s - 1, :], in_=y_vec[g][:, h, s - 1, :]
-                    )
+        def bypass(g, s, h, banks):
+            chans = slice(h * P, (h + 1) * P)
+            byp_ps = banks["byp"].tile([P, GROUP], F32, name="byp_ps")
+            nc.tensor.matmul(
+                out=byp_ps[:],
+                lhsT=byp_w[min(s, 1)][:, chans],
+                rhs=featT_of[(g, s)][:],
+                start=True,
+                stop=True,
+            )
+            byp_sb = work.tile([P, GROUP], F32, name="byp_sb", bufs=5)
+            nc.scalar.mul(out=byp_sb[:], in_=byp_ps[:], mul=math.sqrt(HID / INP))
+            bypass_of[(g, s, h)] = byp_sb
 
-        def norm_scale(stats, kind):
+        def product(g, s, h, banks):
+            chans = slice(h * P, (h + 1) * P)
+            w_codes, w_scales = lin_w[min(s, 1)]
+            codes, scales = operands[(g, s)]
+            mx_ps = banks["mx"].tile([P, GROUP], F32, name="mx_ps")
+            nc.tensor.matmul_mx(
+                out=mx_ps[:],
+                lhsT=w_codes[:, chans].bitcast(FP8X4),
+                lhsT_scale=w_scales[:, chans],
+                rhs=codes[:].bitcast(FP8X4),
+                rhs_scale=scales[:],
+                start=True,
+                stop=True,
+            )
+            mx_of[(g, s, h)] = mx_ps
+
+        def y_of(g, s, h):
+            return y_scal[g][:, h, :] if s == 0 else y_vec[g][:, h, s - 1, :]
+
+        def add(g, s, h):
+            nc.vector.tensor_tensor(
+                out=y_of(g, s, h), in0=bypass_of[(g, s, h)][:], in1=mx_of[(g, s, h)][:], op=ALU.add
+            )
+
+        def gather(g, s, h):
+            if s == 0:
+                nc.vector.bn_stats(out=stats_scal[:, h, g, :], in_=y_of(g, s, h))
+            elif h == 0:
+                nc.vector.bn_stats(out=stats_vec[0][:, g * DV + s - 1, :], in_=y_of(g, s, h))
+            elif s not in SQUARED:
+                nc.vector.bn_stats(out=stats_vec[1][:, g * own + s - 1, :], in_=y_of(g, s, h))
+            else:
+                squared = work.tile([P, GROUP], BF16, name="squared")
+                place = g * len(SQUARED) + SQUARED.index(s)
+                nc.scalar.activation(
+                    out=squared[:],
+                    in_=y_of(g, s, h),
+                    func=ACT.Square,
+                    accum_out=squares[:, place : place + 1],
+                )
+
+        def norm_root(stats, kind):
             moments = consts.tile([P, HALVES, 2], F32, name="moments%d" % kind)
             for h in range(HALVES):
                 nc.vector.bn_aggr(out=moments[:, h, :], in_=stats[h].rearrange("p c s -> p (c s)"))
             spread = consts.tile([P, HALVES], F32, name="spread%d" % kind)
             if kind == 0:
-                nc.vector.tensor_scalar_add(out=spread[:], in0=moments[:, :, 1], scalar1=EPS)
+                nc.vector.tensor_scalar_add(out=spread[:], in0=moments[:, :, 1], scalar1=EPS_HID)
             else:
                 mean_sq = consts.tile([P, HALVES], F32)
                 nc.vector.tensor_mul(out=mean_sq[:], in0=moments[:, :, 0], in1=moments[:, :, 0])
                 nc.vector.scalar_tensor_tensor(
                     out=spread[:],
                     in0=moments[:, :, 1],
-                    scalar=EPS,
+                    scalar=EPS_HID,
                     in1=mean_sq[:],
                     op0=ALU.add,
                     op1=ALU.add,
                 )
+                total = consts.tile([P, 1], F32)
+                nc.vector.reduce_sum(out=total[:], in_=squares[:], axis=mybir.AxisListType.X)
+                rest = consts.tile([P, 1], F32)
+                nc.vector.tensor_scalar(
+                    out=rest[:],
+                    in0=total[:],
+                    scalar1=1.0 / (NODES * DV),
+                    scalar2=EPS_HID * len(SQUARED) / DV,
+                    op0=ALU.mult,
+                    op1=ALU.add,
+                )
+                nc.vector.scalar_tensor_tensor(
+                    out=spread[:, 1:2],
+                    in0=spread[:, 1:2],
+                    scalar=own / DV,
+                    in1=rest[:],
+                    op0=ALU.mult,
+                    op1=ALU.add,
+                )
             root = consts.tile([P, HALVES], F32, name="root%d" % kind)
             nc.scalar.sqrt(out=root[:], in_=spread[:])
+            return moments, root
+
+        def norm_factor(root, kind):
             inverse = consts.tile([P, HALVES], F32, name="inverse%d" % kind)
             nc.vector.reciprocal(out=inverse[:], in_=root[:])
             scale = consts.tile([P, HALVES], F32, name="scale%d" % kind)
             nc.vector.tensor_mul(
                 out=scale[:], in0=inverse[:], in1=bn_cols[:, kind * HALVES : (kind + 1) * HALVES]
             )
-            return moments, scale
+            return scale
 
-        todo = [(0, 0), (1, 0)]
+        units = [(0, 0), (1, 0)]
         for g in range(GROUPS):
-            if g % 2 == 1 and 2 + g // 2 < EARLY:
-                todo.append((2 + g // 2, 0))
-            todo += [(g, s) for s in range(1, SECTIONS)]
-        first_late = len(todo)
-        todo += [(g, 0) for g in range(EARLY, GROUPS)]
+            units += [(g, s) for s in range(1, SECTIONS)]
+            if g in BEHIND:
+                units.append((2 + BEHIND.index(g), 0))
+        n = len(units)
 
         with ExitStack() as part_a:
             vec_in = part_a.enter_context(tc.tile_pool(name="vec_in", bufs=3))
             banks_a = {
-                "x": part_a.enter_context(tc.psum_pool(name="psum_xa", bufs=2)),
-                "f": part_a.enter_context(tc.psum_pool(name="psum_fa", bufs=2)),
+                "x": part_a.enter_context(tc.psum_pool(name="psum_xa", bufs=3)),
+                "f": part_a.enter_context(tc.psum_pool(name="psum_fa", bufs=1)),
                 "mx": part_a.enter_context(tc.psum_pool(name="psum_mxa", bufs=2)),
                 "byp": part_a.enter_context(tc.psum_pool(name="psum_bypa", bufs=2)),
             }
             load_scal(0)
             load_weights(0, lin3_W0, byp_W0)
-            load_scal(1)
-            load_vec(0, vec_in)
+            load_hidden(0, vec_in)
+            load_feat(0, vec_in)
             load_weights(1, lin3_W1, byp_W1)
-            load_vec(1, vec_in)
-            nc.sync.dma_start(out=bn_rows[0:4, :], in_=bn_weight.rearrange("(r c) -> r c", c=P))
-            nc.sync.dma_start(out=bn_rows[4:6, :], in_=bn_bias.rearrange("(r c) -> r c", c=P))
-            ready = prepare(*todo[0], banks_a, vec_in)
-            for i in range(1, first_late):
-                g, s = todo[i]
-                if s == 1 and g + 2 < GROUPS:
-                    load_vec(g + 2, vec_in)
-                    if g % 2 == 0 and 2 + g // 2 < EARLY:
-                        load_scal(2 + g // 2)
-                following = prepare(g, s, banks_a, vec_in)
-                multiply(*todo[i - 1], ready, banks_a)
-                ready = following
-            load_scal(EARLY)
-            load_scal(EARLY + 1)
-            multiply(*todo[first_late - 1], ready, banks_a)
+            load_scal(1)
+            load_hidden(1, vec_in)
+            load_feat(1, vec_in)
+            nc.scalar.dma_start(out=bn_rows[0:4, :], in_=bn_weight.rearrange("(r c) -> r c", c=P))
+            nc.scalar.dma_start(out=bn_rows[4:6, :], in_=bn_bias.rearrange("(r c) -> r c", c=P))
 
-        with ExitStack() as part_b:
-            rows_pool = part_b.enter_context(tc.tile_pool(name="rows", bufs=4))
-            banks_b = {
-                "x": part_b.enter_context(tc.psum_pool(name="psum_xb", bufs=2)),
-                "f": part_b.enter_context(tc.psum_pool(name="psum_fb", bufs=1)),
-                "mx": part_b.enter_context(tc.psum_pool(name="psum_mxb", bufs=1)),
-                "byp": part_b.enter_context(tc.psum_pool(name="psum_bypb", bufs=1)),
-            }
-            psum_out = part_b.enter_context(tc.psum_pool(name="psum_out", bufs=3))
+            for i in range(-SORT_AHEAD, n + STATS_BEHIND):
 
-            bn_ps = banks_b["f"].tile([P, P], BF16, tag="feat_ps")
+                def at(ahead):
+                    return units[i + ahead] if 0 <= i + ahead < n else None
+
+                if at(-1):
+                    add(*at(-1), 0)
+                    add(*at(-1), 1)
+                if at(0):
+                    bypass(*at(0), 0, banks_a)
+                    bypass(*at(0), 1, banks_a)
+                    product(*at(0), 0, banks_a)
+                    product(*at(0), 1, banks_a)
+                if at(2):
+                    g, s = at(2)
+                    turn(g, s, 0, banks_a)
+                    turn(g, s, 1, banks_a)
+                    quantise(g, s)
+                    turn_bypass(g, s, banks_a)
+                    if s == DV and g + 2 < GROUPS:
+                        load_hidden(g + 2, vec_in)
+                        load_feat(g + 2, vec_in)
+                    if s == 0:
+                        load_scal(g + 2)
+                if at(-STATS_BEHIND):
+                    gather(*at(-STATS_BEHIND), 0)
+                    gather(*at(-STATS_BEHIND), 1)
+                if at(SORT_AHEAD) and at(SORT_AHEAD)[1] > 0:
+                    sort(*at(SORT_AHEAD), vec_in)
+
+            bn_ps = banks_a["f"].tile([P, P], BF16, tag="feat_ps")
             nc.tensor.transpose(bn_ps[:], bn_rows[:], ident_bf16[:])
             nc.vector.tensor_copy(out=bn_cols[:], in_=bn_ps[:, 0:6])
+            root_vec = norm_root([stats_vec[0][:], stats_vec[1][:]], 1)[1]
+            scale_vec = norm_factor(root_vec, 1)
 
-            scale_vec = norm_scale([stats_vec[:, 0], stats_vec[:, 1]], 1)[1]
-            scale_ps = psum_out.tile([P, P], F32, tag="vec_ps")
+            scale_ps = banks_a["f"].tile([P, P], F32, tag="feat_ps")
             nc.tensor.matmul(
                 out=scale_ps[:],
                 lhsT=scale_vec[:, 0:1].to_broadcast([P, P]),
@@ -285,6 +356,16 @@ def tile_feedforward_pb_t_kernel(
             )
             scale_row = consts.tile([P, P], F32)
             nc.vector.tensor_copy(out=scale_row[:], in_=scale_ps[:])
+
+        with ExitStack() as part_b:
+            rows_pool = part_b.enter_context(tc.tile_pool(name="rows", bufs=4))
+            banks_b = {
+                "x": part_b.enter_context(tc.psum_pool(name="psum_xb", bufs=1)),
+                "f": part_b.enter_context(tc.psum_pool(name="psum_fb", bufs=1)),
+                "mx": part_b.enter_context(tc.psum_pool(name="psum_mxb", bufs=1)),
+                "byp": part_b.enter_context(tc.psum_pool(name="psum_bypb", bufs=1)),
+            }
+            psum_out = part_b.enter_context(tc.psum_pool(name="psum_out", bufs=4))
 
             def prescale(g, half):
                 nodes = slice(half * GROUP // 2, (half + 1) * GROUP // 2)
@@ -297,78 +378,96 @@ def tile_feedforward_pb_t_kernel(
                     op1=ALU.add,
                 )
 
-            def store_vec(g, half):
-                rows_sb = rows_pool.tile([P, 2, DV * OUTC], F32, name="rows_vec")
-                for jj in range(2):
-                    nodes = slice((2 * half + jj) * P, (2 * half + jj + 1) * P)
-                    for h in range(HALVES):
-                        vec_ps = psum_out.tile([P, DV, P], F32, name="vec_ps")
-                        for d in range(DV):
-                            nc.tensor.transpose(vec_ps[:, d, :], y_vec[g][:, h, d, nodes], ident_f32[:])
-                        dest = rows_sb[:, jj, h * DV * P : (h + 1) * DV * P].rearrange(
-                            "p (o d) -> p o d", d=DV
+            def rows_of(g, half, jj, rows_sb):
+                nodes = slice((2 * half + jj) * P, (2 * half + jj + 1) * P)
+                for h in range(HALVES):
+                    vec_ps = psum_out.tile([P, DV, P], F32, name="vec_ps")
+                    for d in range(DV):
+                        nc.tensor.transpose(vec_ps[:, d, :], y_vec[g][:, h, d, nodes], ident_f32[:])
+                    dest = rows_sb[:, jj, h * DV * P : (h + 1) * DV * P].rearrange(
+                        "p (o d) -> p o d", d=DV
+                    )
+                    if h == 0:
+                        nc.vector.tensor_tensor(
+                            out=dest,
+                            in0=scale_row[:].unsqueeze(2).to_broadcast([P, P, DV]),
+                            in1=vec_ps[:].rearrange("p d o -> p o d"),
+                            op=ALU.mult,
                         )
-                        if h == 0:
-                            nc.vector.tensor_tensor(
-                                out=dest,
-                                in0=vec_ps[:].rearrange("p d o -> p o d"),
-                                in1=scale_row[:].unsqueeze(2).to_broadcast([P, P, DV]),
-                                op=ALU.mult,
-                            )
-                        else:
-                            nc.scalar.copy(out=dest, in_=vec_ps[:].rearrange("p d o -> p o d"))
+                    else:
+                        nc.scalar.copy(out=dest, in_=vec_ps[:].rearrange("p d o -> p o d"))
+
+            def late_step(g, s, k):
+                if k == 0:
+                    turn(g, s, 0, banks_b)
+                elif k == 1:
+                    turn(g, s, 1, banks_b)
+                    turn_bypass(g, s, banks_b)
+                    if g + 2 < GROUPS:
+                        load_scal(g + 2)
+                elif k == 2:
+                    quantise(g, s)
+                    bypass(g, s, 0, banks_b)
+                elif k == 3:
+                    bypass(g, s, 1, banks_b)
+                    product(g, s, 0, banks_b)
+                elif k == 4:
+                    add(g, s, 0)
+                    product(g, s, 1, banks_b)
+                elif k == 5:
+                    gather(g, s, 0)
+                    add(g, s, 1)
+                elif k == 6:
+                    gather(g, s, 1)
+
+            def normalise(g):
+                nc.gpsimd.tensor_scalar(
+                    out=y_scal[g][:, 0, :],
+                    in0=y_scal[g][:, 0, :],
+                    scalar1=scale_scal[:, 0:1],
+                    scalar2=shift[:, 0:1],
+                    op0=ALU.mult,
+                    op1=ALU.add,
+                )
+                nc.scalar.activation(
+                    out=y_scal[g][:, 1, :],
+                    in_=y_scal[g][:, 1, :],
+                    func=ACT.Identity,
+                    scale=scale_scal[:, 1:2],
+                    bias=shift[:, 1:2],
+                )
+
+            late = [(g, 0) for g in range(GROUPS - LATE, GROUPS)]
+            stores = [(g, half) for g in range(GROUPS) for half in range(2)]
+            norm_round = LATE_STEP * (LATE - 1) + 8
+            prescale(*stores[0])
+            prescale(*stores[1])
+            for k, (g, half) in enumerate(stores):
+                if k + 2 < len(stores):
+                    prescale(*stores[k + 2])
+                rows_sb = rows_pool.tile([P, 2, DV * OUTC], F32, name="rows_vec")
+                rows_of(g, half, 0, rows_sb)
+                for w, section in enumerate(late):
+                    late_step(*section, k - 1 - LATE_STEP * w)
+                if k == norm_round:
+                    moments, root_scal = norm_root([stats_scal[:, 0], stats_scal[:, 1]], 0)
+                if k == norm_round + 1:
+                    scale_scal = norm_factor(root_scal, 0)
+                    scaled_mean = consts.tile([P, HALVES], F32)
+                    nc.vector.tensor_mul(out=scaled_mean[:], in0=moments[:, :, 0], in1=scale_scal[:])
+                    shift = consts.tile([P, HALVES], F32)
+                    nc.vector.tensor_sub(
+                        out=shift[:], in0=bn_cols[:, 2 * HALVES : 3 * HALVES], in1=scaled_mean[:]
+                    )
+                rows_of(g, half, 1, rows_sb)
                 group_rows = out[g * GROUP : (g + 1) * GROUP, OUTC:].rearrange("(p j) c -> p j c", j=J)
                 nc.sync.dma_start(out=group_rows[:, 2 * half : 2 * half + 2, :], in_=rows_sb[:])
 
-            stores = [(g, half) for g in range(GROUPS) for half in range(2)]
-            late = len(todo) - first_late
-            prescale(*stores[0])
-            prescale(*stores[1])
-            done = 0
-            ready = None
-            for i in range(late + 1):
-                following = None
-                if i < late:
-                    g = todo[first_late + i][0]
-                    if i >= 1 and g + 1 < GROUPS:
-                        load_scal(g + 1)
-                    following = prepare(*todo[first_late + i], banks_b, None)
-                if ready is not None:
-                    multiply(*todo[first_late + i - 1], ready, banks_b)
-                ready = following
-                until = len(stores) * (i + 1) // (late + 1)
-                while done < until:
-                    if done + 2 < len(stores):
-                        prescale(*stores[done + 2])
-                    store_vec(*stores[done])
-                    done += 1
-
-            moments, scale_scal = norm_scale([stats_scal[:, 0], stats_scal[:, 1]], 0)
-            scaled_mean = consts.tile([P, HALVES], F32)
-            nc.vector.tensor_mul(out=scaled_mean[:], in0=moments[:, :, 0], in1=scale_scal[:])
-            shift = consts.tile([P, HALVES], F32)
-            nc.vector.tensor_sub(
-                out=shift[:], in0=bn_cols[:, 2 * HALVES : 3 * HALVES], in1=scaled_mean[:]
-            )
+            normalise(0)
+            normalise(1)
             for g in range(GROUPS):
-                for h in range(HALVES):
-                    if h == 0:
-                        nc.scalar.activation(
-                            out=y_scal[g][:, h, :],
-                            in_=y_scal[g][:, h, :],
-                            func=ACT.Identity,
-                            scale=scale_scal[:, h : h + 1],
-                            bias=shift[:, h : h + 1],
-                        )
-                    else:
-                        nc.vector.tensor_scalar(
-                            out=y_scal[g][:, h, :],
-                            in0=y_scal[g][:, h, :],
-                            scalar1=scale_scal[:, h : h + 1],
-                            scalar2=shift[:, h : h + 1],
-                            op0=ALU.mult,
-                            op1=ALU.add,
-                        )
+                if g + 2 < GROUPS:
+                    normalise(g + 2)
                 rows_sb = rows_pool.tile([P, J, OUTC], F32, name="rows_scal", bufs=3)
                 for half in range(2):
                     scal_ps = psum_out.tile([P, 2, HALVES, P], F32, tag="vec_ps")

from contextlib import ExitStack
import math

import concourse.mybir as mybir
from concourse.masks import make_identity

F32 = mybir.dt.float32
BF16 = mybir.dt.bfloat16
U32 = mybir.dt.uint32
U8 = mybir.dt.uint8
FP8X4 = mybir.dt.float8_e4m3fn_x4
ALU = mybir.AluOpType
ACT = mybir.ActivationFunctionType

P = 128
NODES = 4096
DV = 3
SECTIONS = 1 + DV
HID = 512
INP = 128
OUTC = 256
HALVES = OUTC // P
GROUP = 512
J = GROUP // P
GROUPS = NODES // GROUP
STATS = 6
EPS = 1e-5
EPS_HID = EPS * HID
SORT_AHEAD = 5
STATS_BEHIND = 5
BEHIND = (1, 3)
LATE = 4
LATE_STEP = 2
SQUARED = (3,)

FLOPS = 2 * NODES * SECTIONS * OUTC * (HID + INP)


def quantise_weight(nc, pool, raw, label):
    grouped = pool.tile([P, OUTC, 4], BF16, name="w_grouped", align_bytes=64, bufs=2)
    nc.vector.tensor_copy(out=grouped[:], in_=raw[:].rearrange("p t c -> p c t"))
    codes = pool.tile([P, OUTC], U32, name=label + "_codes", align_bytes=64)
    scales = pool.tile([P, OUTC], U8, name=label + "_scales", align_bytes=64)
    nc.vector.quantize_mx(
        out=codes[:].bitcast(FP8X4),
        scales=scales[:],
        in_=grouped[:].rearrange("p c t -> p (c t)"),
    )
    return codes, scales


def tile_feedforward_pb_t_kernel(
    tc, h2, features, lin3_W0, lin3_W1, byp_W0, byp_W1, bn_weight, bn_bias, out
):
    nc = tc.nc
    with ExitStack() as whole:
        consts = whole.enter_context(tc.tile_pool(name="consts", bufs=1))
        y_pool = whole.enter_context(tc.tile_pool(name="y", bufs=1))
        scal_in = whole.enter_context(tc.tile_pool(name="scal_in", bufs=2))
        work = whole.enter_context(tc.tile_pool(name="work", bufs=2))

        ident_f32 = consts.tile([P, P], F32)
        make_identity(nc, ident_f32[:])
        ident_bf16 = consts.tile([P, P], BF16)
        make_identity(nc, ident_bf16[:])

        warm = consts.tile([P, 1], F32)
        nc.vector.memset(warm[:], 1.0)
        nc.scalar.sqrt(out=warm[:], in_=warm[:])

        lin_w = {}
        byp_w = {}

        def load_weights(kind, w_hidden, w_bypass):
            raw = consts.tile([P, 4, OUTC], BF16, name="w_raw", bufs=2)
            nc.scalar.dma_start(out=raw[:], in_=w_hidden.rearrange("(p t) c -> p t c", t=4))
            lin_w[kind] = quantise_weight(nc, consts, raw, "w%d" % kind)
            byp_w[kind] = consts.tile([P, OUTC], BF16, name="byp%d" % kind)
            nc.scalar.dma_start(out=byp_w[kind][:], in_=w_bypass)

        bn_rows = consts.tile([P, P], BF16)
        nc.vector.memset(bn_rows[:], 0.0)
        bn_cols = consts.tile([P, 6], F32)

        y_scal = [y_pool.tile([P, HALVES, GROUP], F32, name="ys%d" % g) for g in range(GROUPS)]
        y_vec = [y_pool.tile([P, HALVES, DV, GROUP], F32, name="yv%d" % g) for g in range(GROUPS)]
        own = DV - len(SQUARED)
        stats_scal = consts.tile([P, HALVES, GROUPS, STATS], F32)
        stats_vec = [
            consts.tile([P, GROUPS * DV, STATS], F32, name="stats_vec0"),
            consts.tile([P, GROUPS * own, STATS], F32, name="stats_vec1"),
        ]
        squares = consts.tile([P, GROUPS * len(SQUARED)], F32)

        hidden_of = {}
        feat_of = {}
        sorted_comp = {}
        grouped_of = {}
        operands = {}
        featT_of = {}
        bypass_of = {}
        mx_of = {}

        def load_scal(g):
            rows = slice(g * GROUP, (g + 1) * GROUP)
            hidden = scal_in.tile([P, J, HID], BF16, name="h2_scal")
            nc.sync.dma_start(
                out=hidden[:], in_=h2[rows, 0:HID].rearrange("(p j) k -> p j k", j=J)
            )
            feat = scal_in.tile([P, J, INP], BF16, name="feat_scal")
            nc.sync.dma_start(
                out=feat[:], in_=features[rows, 0:INP].rearrange("(p j) k -> p j k", j=J)
            )
            hidden_of[(g, 0)] = hidden
            feat_of[(g, 0)] = feat

        def load_hidden(g, vec_in):
            rows = h2[g * GROUP : (g + 1) * GROUP, HID:].rearrange("(p j) k -> p j k", j=J)
            hidden = vec_in.tile([P, J, DV * HID], BF16, name="h2_vec", bufs=2)
            nc.sync.dma_start(out=hidden[:], in_=rows)
            hidden_of.update({(g, s): hidden for s in range(1, SECTIONS)})

        def load_feat(g, vec_in):
            rows = features[g * GROUP : (g + 1) * GROUP, INP:].rearrange("(p j) k -> p j k", j=J)
            feat = vec_in.tile([P, J, DV * INP], BF16, name="feat_vec")
            nc.sync.dma_start(out=feat[:], in_=rows)
            feat_of.update({(g, s): feat for s in range(1, SECTIONS)})

        def sort(g, s, vec_in):
            comp = vec_in.tile([P, J, HID], BF16, name="h2_comp")
            for half in range(2):
                pair = slice(2 * half, 2 * half + 2)
                nc.gpsimd.tensor_scalar(
                    out=comp[:, pair, :],
                    in0=hidden_of[(g, s)][:, pair, :].rearrange("p j (i d) -> p d j i", d=DV)[:, s - 1],
                    scalar1=1.0,
                    scalar2=0.0,
                    op0=ALU.mult,
                    op1=ALU.add,
                )
            sorted_comp[(g, s)] = comp

        def turn(g, s, half, banks):
            if half == 0:
                grouped_of[(g, s)] = work.tile([P, GROUP, 4], BF16, name="grouped", align_bytes=64)
            dest = grouped_of[(g, s)][:, half * 2 * P : (half + 1) * 2 * P, :]
            hidden = hidden_of[(g, s)] if s == 0 else sorted_comp[(g, s)]
            hid_ps = banks["x"].tile([P, 2, 2 * P], F32, name="hid_ps")
            for jj in range(2):
                words = hidden[:, 2 * half + jj, :].bitcast(F32)
                for u in range(2):
                    nc.tensor.transpose(
                        hid_ps[:, u, jj * P : (jj + 1) * P], words[:, u::2], ident_f32[:]
                    )
            nc.scalar.copy(
                out=dest.rearrange("p n t -> p (n t)").bitcast(F32).rearrange("p (n u) -> p n u", u=2),
                in_=hid_ps[:].rearrange("p u n -> p n u"),
            )

        def quantise(g, s):
            codes = work.tile([P, GROUP], U32, name="codes", align_bytes=64, bufs=3)
            scales = work.tile([P, GROUP], U8, name="scales", align_bytes=64, bufs=3)
            nc.vector.quantize_mx(
                out=codes[:].bitcast(FP8X4),
                scales=scales[:],
                in_=grouped_of[(g, s)][:].rearrange("p n t -> p (n t)"),
            )
            operands[(g, s)] = (codes, scales)

        def turn_bypass(g, s, banks):
            feat = feat_of[(g, s)]
            feat_ps = banks["f"].tile([P, GROUP], BF16, name="feat_ps")
            for j in range(J):
                cols = feat[:, j, :]
                if s > 0:
                    cols = cols.rearrange("p (i d) -> p d i", d=DV)[:, s - 1]
                nc.tensor.transpose(feat_ps[:, j * P : (j + 1) * P], cols, ident_bf16[:])
            featT = work.tile([P, GROUP], BF16, name="featT", bufs=4)
            nc.scalar.copy(out=featT[:], in_=feat_ps[:])
            featT_of[(g, s)] = featT

        def bypass(g, s, h, banks):
            chans = slice(h * P, (h + 1) * P)
            byp_ps = banks["byp"].tile([P, GROUP], F32, name="byp_ps")
            nc.tensor.matmul(
                out=byp_ps[:],
                lhsT=byp_w[min(s, 1)][:, chans],
                rhs=featT_of[(g, s)][:],
                start=True,
                stop=True,
            )
            byp_sb = work.tile([P, GROUP], F32, name="byp_sb", bufs=5)
            nc.scalar.mul(out=byp_sb[:], in_=byp_ps[:], mul=math.sqrt(HID / INP))
            bypass_of[(g, s, h)] = byp_sb

        def product(g, s, h, banks):
            chans = slice(h * P, (h + 1) * P)
            w_codes, w_scales = lin_w[min(s, 1)]
            codes, scales = operands[(g, s)]
            mx_ps = banks["mx"].tile([P, GROUP], F32, name="mx_ps")
            nc.tensor.matmul_mx(
                out=mx_ps[:],
                lhsT=w_codes[:, chans].bitcast(FP8X4),
                lhsT_scale=w_scales[:, chans],
                rhs=codes[:].bitcast(FP8X4),
                rhs_scale=scales[:],
                start=True,
                stop=True,
            )
            mx_of[(g, s, h)] = mx_ps

        def y_of(g, s, h):
            return y_scal[g][:, h, :] if s == 0 else y_vec[g][:, h, s - 1, :]

        def add(g, s, h):
            nc.vector.tensor_tensor(
                out=y_of(g, s, h), in0=bypass_of[(g, s, h)][:], in1=mx_of[(g, s, h)][:], op=ALU.add
            )

        def gather(g, s, h):
            if s == 0:
                nc.vector.bn_stats(out=stats_scal[:, h, g, :], in_=y_of(g, s, h))
            elif h == 0:
                nc.vector.bn_stats(out=stats_vec[0][:, g * DV + s - 1, :], in_=y_of(g, s, h))
            elif s not in SQUARED:
                nc.vector.bn_stats(out=stats_vec[1][:, g * own + s - 1, :], in_=y_of(g, s, h))
            else:
                squared = work.tile([P, GROUP], BF16, name="squared")
                place = g * len(SQUARED) + SQUARED.index(s)
                nc.scalar.activation(
                    out=squared[:],
                    in_=y_of(g, s, h),
                    func=ACT.Square,
                    accum_out=squares[:, place : place + 1],
                )

        def norm_root(stats, kind):
            moments = consts.tile([P, HALVES, 2], F32, name="moments%d" % kind)
            for h in range(HALVES):
                nc.vector.bn_aggr(out=moments[:, h, :], in_=stats[h].rearrange("p c s -> p (c s)"))
            spread = consts.tile([P, HALVES], F32, name="spread%d" % kind)
            if kind == 0:
                nc.vector.tensor_scalar_add(out=spread[:], in0=moments[:, :, 1], scalar1=EPS_HID)
            else:
                mean_sq = consts.tile([P, HALVES], F32)
                nc.vector.tensor_mul(out=mean_sq[:], in0=moments[:, :, 0], in1=moments[:, :, 0])
                nc.vector.scalar_tensor_tensor(
                    out=spread[:],
                    in0=moments[:, :, 1],
                    scalar=EPS_HID,
                    in1=mean_sq[:],
                    op0=ALU.add,
                    op1=ALU.add,
                )
                total = consts.tile([P, 1], F32)
                nc.vector.reduce_sum(out=total[:], in_=squares[:], axis=mybir.AxisListType.X)
                rest = consts.tile([P, 1], F32)
                nc.vector.tensor_scalar(
                    out=rest[:],
                    in0=total[:],
                    scalar1=1.0 / (NODES * DV),
                    scalar2=EPS_HID * len(SQUARED) / DV,
                    op0=ALU.mult,
                    op1=ALU.add,
                )
                nc.vector.scalar_tensor_tensor(
                    out=spread[:, 1:2],
                    in0=spread[:, 1:2],
                    scalar=own / DV,
                    in1=rest[:],
                    op0=ALU.mult,
                    op1=ALU.add,
                )
            root = consts.tile([P, HALVES], F32, name="root%d" % kind)
            nc.scalar.sqrt(out=root[:], in_=spread[:])
            return moments, root

        def norm_factor(root, kind):
            inverse = consts.tile([P, HALVES], F32, name="inverse%d" % kind)
            nc.vector.reciprocal(out=inverse[:], in_=root[:])
            scale = consts.tile([P, HALVES], F32, name="scale%d" % kind)
            nc.vector.tensor_mul(
                out=scale[:], in0=inverse[:], in1=bn_cols[:, kind * HALVES : (kind + 1) * HALVES]
            )
            return scale

        units = [(0, 0), (1, 0)]
        for g in range(GROUPS):
            units += [(g, s) for s in range(1, SECTIONS)]
            if g in BEHIND:
                units.append((2 + BEHIND.index(g), 0))
        n = len(units)

        with ExitStack() as part_a:
            vec_in = part_a.enter_context(tc.tile_pool(name="vec_in", bufs=3))
            banks_a = {
                "x": part_a.enter_context(tc.psum_pool(name="psum_xa", bufs=3)),
                "f": part_a.enter_context(tc.psum_pool(name="psum_fa", bufs=1)),
                "mx": part_a.enter_context(tc.psum_pool(name="psum_mxa", bufs=2)),
                "byp": part_a.enter_context(tc.psum_pool(name="psum_bypa", bufs=2)),
            }
            load_scal(0)
            load_weights(0, lin3_W0, byp_W0)
            load_hidden(0, vec_in)
            load_feat(0, vec_in)
            load_weights(1, lin3_W1, byp_W1)
            load_scal(1)
            load_hidden(1, vec_in)
            load_feat(1, vec_in)
            nc.scalar.dma_start(out=bn_rows[0:4, :], in_=bn_weight.rearrange("(r c) -> r c", c=P))
            nc.scalar.dma_start(out=bn_rows[4:6, :], in_=bn_bias.rearrange("(r c) -> r c", c=P))

            for i in range(-SORT_AHEAD, n + STATS_BEHIND):

                def at(ahead):
                    return units[i + ahead] if 0 <= i + ahead < n else None

                if at(-1):
                    add(*at(-1), 0)
                    add(*at(-1), 1)
                if at(0):
                    bypass(*at(0), 0, banks_a)
                    bypass(*at(0), 1, banks_a)
                    product(*at(0), 0, banks_a)
                    product(*at(0), 1, banks_a)
                if at(2):
                    g, s = at(2)
                    turn(g, s, 0, banks_a)
                    turn(g, s, 1, banks_a)
                    quantise(g, s)
                    turn_bypass(g, s, banks_a)
                    if s == DV and g + 2 < GROUPS:
                        load_hidden(g + 2, vec_in)
                        load_feat(g + 2, vec_in)
                    if s == 0:
                        load_scal(g + 2)
                if at(-STATS_BEHIND):
                    gather(*at(-STATS_BEHIND), 0)
                    gather(*at(-STATS_BEHIND), 1)
                if at(SORT_AHEAD) and at(SORT_AHEAD)[1] > 0:
                    sort(*at(SORT_AHEAD), vec_in)

            bn_ps = banks_a["f"].tile([P, P], BF16, tag="feat_ps")
            nc.tensor.transpose(bn_ps[:], bn_rows[:], ident_bf16[:])
            nc.vector.tensor_copy(out=bn_cols[:], in_=bn_ps[:, 0:6])
            root_vec = norm_root([stats_vec[0][:], stats_vec[1][:]], 1)[1]
            scale_vec = norm_factor(root_vec, 1)

            scale_ps = banks_a["f"].tile([P, P], F32, tag="feat_ps")
            nc.tensor.matmul(
                out=scale_ps[:],
                lhsT=scale_vec[:, 0:1].to_broadcast([P, P]),
                rhs=ident_f32[:],
                start=True,
                stop=True,
            )
            scale_row = consts.tile([P, P], F32)
            nc.vector.tensor_copy(out=scale_row[:], in_=scale_ps[:])

        with ExitStack() as part_b:
            rows_pool = part_b.enter_context(tc.tile_pool(name="rows", bufs=4))
            banks_b = {
                "x": part_b.enter_context(tc.psum_pool(name="psum_xb", bufs=1)),
                "f": part_b.enter_context(tc.psum_pool(name="psum_fb", bufs=1)),
                "mx": part_b.enter_context(tc.psum_pool(name="psum_mxb", bufs=1)),
                "byp": part_b.enter_context(tc.psum_pool(name="psum_bypb", bufs=1)),
            }
            psum_out = part_b.enter_context(tc.psum_pool(name="psum_out", bufs=4))

            def prescale(g, half):
                nodes = slice(half * GROUP // 2, (half + 1) * GROUP // 2)
                nc.gpsimd.tensor_scalar(
                    out=y_vec[g][:, 1, :, nodes],
                    in0=y_vec[g][:, 1, :, nodes],
                    scalar1=scale_vec[:, 1:2],
                    scalar2=0.0,
                    op0=ALU.mult,
                    op1=ALU.add,
                )

            def rows_of(g, half, jj, rows_sb):
                nodes = slice((2 * half + jj) * P, (2 * half + jj + 1) * P)
                for h in range(HALVES):
                    vec_ps = psum_out.tile([P, DV, P], F32, name="vec_ps")
                    for d in range(DV):
                        nc.tensor.transpose(vec_ps[:, d, :], y_vec[g][:, h, d, nodes], ident_f32[:])
                    dest = rows_sb[:, jj, h * DV * P : (h + 1) * DV * P].rearrange(
                        "p (o d) -> p o d", d=DV
                    )
                    if h == 0:
                        nc.vector.tensor_tensor(
                            out=dest,
                            in0=scale_row[:].unsqueeze(2).to_broadcast([P, P, DV]),
                            in1=vec_ps[:].rearrange("p d o -> p o d"),
                            op=ALU.mult,
                        )
                    else:
                        nc.scalar.copy(out=dest, in_=vec_ps[:].rearrange("p d o -> p o d"))

            def late_step(g, s, k):
                if k == 0:
                    turn(g, s, 0, banks_b)
                elif k == 1:
                    turn(g, s, 1, banks_b)
                    turn_bypass(g, s, banks_b)
                    if g + 2 < GROUPS:
                        load_scal(g + 2)
                elif k == 2:
                    quantise(g, s)
                    bypass(g, s, 0, banks_b)
                elif k == 3:
                    bypass(g, s, 1, banks_b)
                    product(g, s, 0, banks_b)
                elif k == 4:
                    add(g, s, 0)
                    product(g, s, 1, banks_b)
                elif k == 5:
                    gather(g, s, 0)
                    add(g, s, 1)
                elif k == 6:
                    gather(g, s, 1)

            def normalise(g):
                nc.gpsimd.tensor_scalar(
                    out=y_scal[g][:, 0, :],
                    in0=y_scal[g][:, 0, :],
                    scalar1=scale_scal[:, 0:1],
                    scalar2=shift[:, 0:1],
                    op0=ALU.mult,
                    op1=ALU.add,
                )
                nc.scalar.activation(
                    out=y_scal[g][:, 1, :],
                    in_=y_scal[g][:, 1, :],
                    func=ACT.Identity,
                    scale=scale_scal[:, 1:2],
                    bias=shift[:, 1:2],
                )

            late = [(g, 0) for g in range(GROUPS - LATE, GROUPS)]
            stores = [(g, half) for g in range(GROUPS) for half in range(2)]
            norm_round = LATE_STEP * (LATE - 1) + 8
            prescale(*stores[0])
            prescale(*stores[1])
            for k, (g, half) in enumerate(stores):
                if k + 2 < len(stores):
                    prescale(*stores[k + 2])
                rows_sb = rows_pool.tile([P, 2, DV * OUTC], F32, name="rows_vec")
                rows_of(g, half, 0, rows_sb)
                for w, section in enumerate(late):
                    late_step(*section, k - 1 - LATE_STEP * w)
                if k == norm_round:
                    moments, root_scal = norm_root([stats_scal[:, 0], stats_scal[:, 1]], 0)
                if k == norm_round + 1:
                    scale_scal = norm_factor(root_scal, 0)
                    scaled_mean = consts.tile([P, HALVES], F32)
                    nc.vector.tensor_mul(out=scaled_mean[:], in0=moments[:, :, 0], in1=scale_scal[:])
                    shift = consts.tile([P, HALVES], F32)
                    nc.vector.tensor_sub(
                        out=shift[:], in0=bn_cols[:, 2 * HALVES : 3 * HALVES], in1=scaled_mean[:]
                    )
                rows_of(g, half, 1, rows_sb)
                group_rows = out[g * GROUP : (g + 1) * GROUP, OUTC:].rearrange("(p j) c -> p j c", j=J)
                nc.sync.dma_start(out=group_rows[:, 2 * half : 2 * half + 2, :], in_=rows_sb[:])

            normalise(0)
            normalise(1)
            for g in range(GROUPS):
                if g + 2 < GROUPS:
                    normalise(g + 2)
                rows_sb = rows_pool.tile([P, J, OUTC], F32, name="rows_scal", bufs=3)
                for half in range(2):
                    scal_ps = psum_out.tile([P, 2, HALVES, P], F32, tag="vec_ps")
                    for jj in range(2):
                        nodes = slice((2 * half + jj) * P, (2 * half + jj + 1) * P)
                        for h in range(HALVES):
                            nc.tensor.transpose(scal_ps[:, jj, h, :], y_scal[g][:, h, nodes], ident_f32[:])
                    dest = rows_sb[:, 2 * half : 2 * half + 2, :]
                    flat = scal_ps[:].rearrange("p j h c -> p j (h c)")
                    if half == 0:
                        nc.scalar.copy(out=dest, in_=flat)
                    else:
                        nc.vector.tensor_copy(out=dest, in_=flat)
                group_rows = out[g * GROUP : (g + 1) * GROUP, 0:OUTC].rearrange("(p j) c -> p j c", j=J)
                nc.sync.dma_start(out=group_rows, in_=rows_sb[:])
